import numpy as np
import ml_dtypes


def mxq(x, axis, fmt="e4m3"):
    dtype, down = {"e4m3": (ml_dtypes.float8_e4m3fn, 7), "e5m2": (ml_dtypes.float8_e5m2, 14)}[fmt]
    v = np.moveaxis(np.asarray(x, np.float32).astype(ml_dtypes.bfloat16).astype(np.float64), axis, -1)
    blocks = v.reshape(v.shape[:-1] + (-1, 32))
    amax = np.abs(blocks).max(-1, keepdims=True)
    byte = np.maximum(np.where(amax > 0, np.frexp(amax)[1] - 1 + 127, 0) - down, 1)
    scale = np.exp2(byte - 127.0)
    codes = (blocks / scale).astype(np.float32).astype(dtype).astype(np.float64)
    return np.moveaxis((codes * scale).reshape(v.shape), -1, axis)


WIDE = False


def mx_kscale(k):
    if not WIDE:
        return np.ones(k)
    levels = np.array([10, -10, 5, -5, 0])
    a = np.random.permutation(np.resize(levels, k // 512 * 4)).reshape(k // 512, 4)
    idx = np.arange(k)
    return np.exp2(a[idx // 512, idx % 128 // 32])


BF16 = ml_dtypes.bfloat16


def bf(x):
    return np.asarray(x, np.float32).astype(BF16)


def f64(x):
    return np.asarray(x).astype(np.float64)


N1, N2, N3, R1, R = 128, 128, 128, 512, 1024


def setup_inputs():
    s = mx_kscale(R)
    g = R ** (-1.0 / 6.0)
    return {"X": bf(np.random.standard_normal((N1, N2, N3))),
            "A": bf(np.random.standard_normal((N1, R)) * g * s),
            "B": bf(np.random.standard_normal((N2, R)) * g),
            "C": bf(np.random.standard_normal((N3, R)) * g / s)}


def reference(X, A, B, C):
    p = (f64(A)[:, None, :] * f64(B)[None, :, :]).reshape(N1 * N2, R)
    approx = mxq(p, 1, "e4m3") @ mxq(f64(C), 1, "e4m3").T
    return approx.reshape(N1, N2, N3) - f64(X)

@@ -1,0 +1,141 @@
+import concourse.mybir as mybir
+from concourse.masks import make_identity
+
+BF16 = mybir.dt.bfloat16
+F32 = mybir.dt.float32
+U32 = mybir.dt.uint32
+U8 = mybir.dt.uint8
+FP8X4 = mybir.dt.float8_e4m3fn_x4
+
+P = 128
+PACK = 4
+K_PASS = P * PACK
+N1 = 128
+N2 = 128
+N3 = 128
+R = 1024
+PASSES = R // K_PASS
+PAIRS = PACK // 2
+
+J_GROUP = 4
+GROUPS = N2 // J_GROUP
+GROUP_WORDS = J_GROUP * N1
+X_CHUNK_J = 16
+X_CHUNKS = N2 // X_CHUNK_J
+
+FLOPS = 2 * N1 * N2 * N3 * R
+
+
+def turn_factor(nc, psum, ident, raw, copy, turned):
+    words = raw[:].bitcast(F32).rearrange("row (g p u) -> row g u p", g=PASSES, u=PAIRS)
+    flipped = psum.tile([P, PASSES, PAIRS, P], F32)
+    for g in range(PASSES):
+        for u in range(PAIRS):
+            nc.tensor.transpose(flipped[:, g, u, :], words[:, g, u, :], ident[:])
+    copy(
+        out=turned[:].bitcast(F32).rearrange("p (g row u) -> p g row u", g=PASSES, u=PAIRS),
+        in_=flipped[:].rearrange("p g u row -> p g row u"),
+    )
+
+
+def tile_recon_loss_pa_t_kernel(tc, X, A, B, C, out):
+    nc = tc.nc
+    x_rows = X.rearrange("i j k -> i (j k)")
+    out_rows = out.rearrange("i j k -> i (j k)")
+
+    with tc.tile_pool(name="keep", bufs=1) as keep, tc.tile_pool(
+        name="work", bufs=3
+    ) as work, tc.psum_pool(name="turn", bufs=2) as turn_psum, tc.psum_pool(
+        name="sums", bufs=3
+    ) as sums_psum:
+        a_raw = keep.tile([P, R], BF16)
+        b_raw = keep.tile([P, R], BF16)
+        c_raw = keep.tile([P, R], BF16)
+        nc.sync.dma_start(out=a_raw[:], in_=A[:, :])
+        nc.scalar.dma_start(out=b_raw[:], in_=B[:, :])
+        nc.sync.dma_start(out=c_raw[:], in_=C[:, :])
+        x_chunks = []
+        for c in range(X_CHUNKS):
+            x_chunk = keep.tile([P, X_CHUNK_J * N3], BF16, name="x_chunk%d" % c)
+            cols = slice(c * X_CHUNK_J * N3, (c + 1) * X_CHUNK_J * N3)
+            nc.sync.dma_start(out=x_chunk[:], in_=x_rows[:, cols])
+            x_chunks.append(x_chunk)
+
+        ident = keep.tile([P, P], F32)
+        make_identity(nc, ident[:])
+
+        a_turned = keep.tile([P, PASSES * N1 * PACK], BF16)
+        b_turned = keep.tile([P, PASSES * N2 * PACK], BF16)
+        c_turned = keep.tile([P, PASSES * N3 * PACK], BF16, align_bytes=64)
+        turn_factor(nc, turn_psum, ident, a_raw, nc.vector.tensor_copy, a_turned)
+        turn_factor(nc, turn_psum, ident, b_raw, nc.scalar.copy, b_turned)
+        turn_factor(nc, turn_psum, ident, c_raw, nc.scalar.copy, c_turned)
+        a_view = a_turned[:].rearrange("p (g i t) -> p g i t", g=PASSES, t=PACK)
+        b_view = b_turned[:].rearrange("p (g j t) -> p g j t", g=PASSES, t=PACK)
+
+        c_codes = keep.tile([P, PASSES * N3], U32, align_bytes=64)
+        c_scales = keep.tile([P, PASSES * N3], U8, align_bytes=64)
+
+        def multiply_and_quantise(n):
+            j_rows = slice(n * J_GROUP, (n + 1) * J_GROUP)
+            shape = [P, J_GROUP, N1, PACK]
+            products = []
+            for g in range(PASSES):
+                product = work.tile([P, GROUP_WORDS * PACK], BF16, align_bytes=64, name="product%d" % g)
+                nc.vector.tensor_tensor(
+                    out=product[:].rearrange("p (j i t) -> p j i t", j=J_GROUP, t=PACK),
+                    in0=a_view[:, g, :, :].unsqueeze(1).to_broadcast(shape),
+                    in1=b_view[:, g, j_rows, :].unsqueeze(2).to_broadcast(shape),
+                    op=mybir.AluOpType.mult,
+                )
+                products.append(product)
+            codes = work.tile([P, PASSES, GROUP_WORDS], U32, align_bytes=64)
+            scales = work.tile([P, PASSES, GROUP_WORDS], U8, align_bytes=64)
+            for g in range(PASSES):
+                nc.vector.quantize_mx(
+                    out=codes[:, g, :].bitcast(FP8X4), scales=scales[:, g, :], in_=products[g][:]
+                )
+            return codes, scales
+
+        def contract(codes, scales):
+            sums = sums_psum.tile([P, J_GROUP, N3], F32)
+            for j in range(J_GROUP):
+                i_cols = slice(j * N1, (j + 1) * N1)
+                for g in range(PASSES):
+                    k_cols = slice(g * N3, (g + 1) * N3)
+                    nc.tensor.matmul_mx(
+                        out=sums[:, j, :],
+                        lhsT=codes[:, g, i_cols].bitcast(FP8X4),
+                        lhsT_scale=scales[:, g, i_cols],
+                        rhs=c_codes[:, k_cols].bitcast(FP8X4),
+                        rhs_scale=c_scales[:, k_cols],
+                        start=(g == 0),
+                        stop=(g == PASSES - 1),
+                    )
+            return sums
+
+        def subtract_and_store(n, sums):
+            width = J_GROUP * N3
+            first = (n * J_GROUP % X_CHUNK_J) * N3
+            x_part = x_chunks[n * J_GROUP // X_CHUNK_J][:, first : first + width]
+            residual = work.tile([P, width], F32)
+            nc.vector.tensor_tensor(
+                out=residual[:],
+                in0=sums[:].rearrange("p j k -> p (j k)"),
+                in1=x_part,
+                op=mybir.AluOpType.subtract,
+            )
+            nc.sync.dma_start(out=out_rows[:, n * width : (n + 1) * width], in_=residual[:])
+
+        waiting = None
+        for n in range(GROUPS):
+            codes, scales = multiply_and_quantise(n)
+            if n == 0:
+                nc.vector.quantize_mx(
+                    out=c_codes[:].bitcast(FP8X4), scales=c_scales[:], in_=c_turned[:]
+                )
+            sums = contract(codes, scales)
+            if waiting is not None:
+                subtract_and_store(n - 1, waiting)
+            waiting = sums
+        subtract_and_store(GROUPS - 1, waiting)

@@ -20,6 +20,7 @@ PAIRS = PACK // 2
 J_GROUP = 4
 GROUPS = N2 // J_GROUP
 GROUP_WORDS = J_GROUP * N1
+SCALAR_EVERY = 4
 X_CHUNK_J = 16
 X_CHUNKS = N2 // X_CHUNK_J
 
@@ -45,7 +46,7 @@ def tile_recon_loss_pa_t_kernel(tc, X, A, B, C, out):
 
     with tc.tile_pool(name="keep", bufs=1) as keep, tc.tile_pool(
         name="work", bufs=3
-    ) as work, tc.psum_pool(name="turn", bufs=2) as turn_psum, tc.psum_pool(
+    ) as work, tc.tile_pool(name="scalar_work", bufs=2) as scalar_work, tc.psum_pool(name="turn", bufs=2) as turn_psum, tc.psum_pool(
         name="sums", bufs=3
     ) as sums_psum:
         a_raw = keep.tile([P, R], BF16)
@@ -73,22 +74,47 @@ def tile_recon_loss_pa_t_kernel(tc, X, A, B, C, out):
         a_view = a_turned[:].rearrange("p (g i t) -> p g i t", g=PASSES, t=PACK)
         b_view = b_turned[:].rearrange("p (g j t) -> p g j t", g=PASSES, t=PACK)
 
+        b_float = keep.tile([P, PASSES * N2 * PACK], F32)
+        nc.scalar.copy(out=b_float[:], in_=b_turned[:])
+        b_float_view = b_float[:].rearrange("p (g j t) -> p g j t", g=PASSES, t=PACK)
+
         c_codes = keep.tile([P, PASSES * N3], U32, align_bytes=64)
         c_scales = keep.tile([P, PASSES * N3], U8, align_bytes=64)
 
-        def multiply_and_quantise(n):
+        def multiply_on_vector(n, g):
             j_rows = slice(n * J_GROUP, (n + 1) * J_GROUP)
             shape = [P, J_GROUP, N1, PACK]
-            products = []
-            for g in range(PASSES):
-                product = work.tile([P, GROUP_WORDS * PACK], BF16, align_bytes=64, name="product%d" % g)
-                nc.vector.tensor_tensor(
-                    out=product[:].rearrange("p (j i t) -> p j i t", j=J_GROUP, t=PACK),
-                    in0=a_view[:, g, :, :].unsqueeze(1).to_broadcast(shape),
-                    in1=b_view[:, g, j_rows, :].unsqueeze(2).to_broadcast(shape),
-                    op=mybir.AluOpType.mult,
-                )
-                products.append(product)
+            product = work.tile([P, GROUP_WORDS * PACK], BF16, align_bytes=64, name="product%d" % g)
+            nc.vector.tensor_tensor(
+                out=product[:].rearrange("p (j i t) -> p j i t", j=J_GROUP, t=PACK),
+                in0=a_view[:, g, :, :].unsqueeze(1).to_broadcast(shape),
+                in1=b_view[:, g, j_rows, :].unsqueeze(2).to_broadcast(shape),
+                op=mybir.AluOpType.mult,
+            )
+            return product
+
+        def multiply_on_scalar(n, g):
+            planes = scalar_work.tile([P, J_GROUP, PACK, N1], BF16)
+            for j in range(J_GROUP):
+                for t in range(PACK):
+                    nc.scalar.activation(
+                        out=planes[:, j, t, :],
+                        in_=a_view[:, g, :, t],
+                        func=mybir.ActivationFunctionType.Copy,
+                        scale=b_float_view[:, g, n * J_GROUP + j, t : t + 1],
+                    )
+            product = scalar_work.tile(
+                [P, GROUP_WORDS * PACK], BF16, align_bytes=64, name="scalar_product%d" % g
+            )
+            nc.scalar.copy(
+                out=product[:].rearrange("p (j i t) -> p j i t", j=J_GROUP, t=PACK),
+                in_=planes[:].rearrange("p j t i -> p j i t"),
+            )
+            return product
+
+        def multiply_and_quantise(n):
+            multiply = multiply_on_scalar if n % SCALAR_EVERY == SCALAR_EVERY - 1 else multiply_on_vector
+            products = [multiply(n, g) for g in range(PASSES)]
             codes = work.tile([P, PASSES, GROUP_WORDS], U32, align_bytes=64)
             scales = work.tile([P, PASSES, GROUP_WORDS], U8, align_bytes=64)
             for g in range(PASSES):

@@ -19,7 +19,8 @@ PAIRS = PACK // 2
 
 J_GROUP = 4
 GROUPS = N2 // J_GROUP
-GROUP_WORDS = J_GROUP * N1
+GROUP_WORDS = J_GROUP * PASSES * N1
+GROUP_COLS = GROUP_WORDS * PACK
 SCALAR_EVERY = 4
 X_CHUNK_J = 16
 X_CHUNKS = N2 // X_CHUNK_J
@@ -27,16 +28,13 @@ X_CHUNKS = N2 // X_CHUNK_J
 FLOPS = 2 * N1 * N2 * N3 * R
 
 
-def turn_factor(nc, psum, ident, raw, copy, turned):
+def turn_factor(nc, psum, ident, raw, copy, turned_words):
     words = raw[:].bitcast(F32).rearrange("row (g p u) -> row g u p", g=PASSES, u=PAIRS)
     flipped = psum.tile([P, PASSES, PAIRS, P], F32)
     for g in range(PASSES):
         for u in range(PAIRS):
             nc.tensor.transpose(flipped[:, g, u, :], words[:, g, u, :], ident[:])
-    copy(
-        out=turned[:].bitcast(F32).rearrange("p (g row u) -> p g row u", g=PASSES, u=PAIRS),
-        in_=flipped[:].rearrange("p g u row -> p g row u"),
-    )
+    copy(out=turned_words, in_=flipped[:].rearrange("p g u row -> p g row u"))
 
 
 def tile_recon_loss_pa_t_kernel(tc, X, A, B, C, out):
@@ -44,11 +42,11 @@ def tile_recon_loss_pa_t_kernel(tc, X, A, B, C, out):
     x_rows = X.rearrange("i j k -> i (j k)")
     out_rows = out.rearrange("i j k -> i (j k)")
 
-    with tc.tile_pool(name="keep", bufs=1) as keep, tc.tile_pool(
-        name="work", bufs=3
-    ) as work, tc.tile_pool(name="scalar_work", bufs=2) as scalar_work, tc.psum_pool(name="turn", bufs=2) as turn_psum, tc.psum_pool(
-        name="sums", bufs=3
-    ) as sums_psum:
+    with tc.tile_pool(name="keep", bufs=1) as keep, tc.tile_pool(name="work", bufs=3) as work, tc.tile_pool(
+        name="products", bufs=2
+    ) as products, tc.tile_pool(name="scalar_work", bufs=2) as scalar_work, tc.psum_pool(
+        name="turn", bufs=2
+    ) as turn_psum, tc.psum_pool(name="sums", bufs=3) as sums_psum, tc.manual_schedule():
         a_raw = keep.tile([P, R], BF16)
         b_raw = keep.tile([P, R], BF16)
         c_raw = keep.tile([P, R], BF16)
@@ -66,73 +64,76 @@ def tile_recon_loss_pa_t_kernel(tc, X, A, B, C, out):
         make_identity(nc, ident[:])
 
         a_turned = keep.tile([P, PASSES * N1 * PACK], BF16)
-        b_turned = keep.tile([P, PASSES * N2 * PACK], BF16)
+        b_turned = keep.tile([P, N2 * PASSES * PACK], BF16)
         c_turned = keep.tile([P, PASSES * N3 * PACK], BF16, align_bytes=64)
-        turn_factor(nc, turn_psum, ident, a_raw, nc.vector.tensor_copy, a_turned)
-        turn_factor(nc, turn_psum, ident, b_raw, nc.scalar.copy, b_turned)
-        turn_factor(nc, turn_psum, ident, c_raw, nc.scalar.copy, c_turned)
+        turn_factor(
+            nc, turn_psum, ident, a_raw, nc.vector.tensor_copy,
+            a_turned[:].bitcast(F32).rearrange("p (g row u) -> p g row u", g=PASSES, u=PAIRS),
+        )
+        turn_factor(
+            nc, turn_psum, ident, b_raw, nc.scalar.copy,
+            b_turned[:].bitcast(F32).rearrange("p (row g u) -> p g row u", g=PASSES, u=PAIRS),
+        )
+        turn_factor(
+            nc, turn_psum, ident, c_raw, nc.scalar.copy,
+            c_turned[:].bitcast(F32).rearrange("p (g row u) -> p g row u", g=PASSES, u=PAIRS),
+        )
         a_view = a_turned[:].rearrange("p (g i t) -> p g i t", g=PASSES, t=PACK)
-        b_view = b_turned[:].rearrange("p (g j t) -> p g j t", g=PASSES, t=PACK)
+        b_view = b_turned[:].rearrange("p (j g t) -> p j g t", g=PASSES, t=PACK)
 
-        b_float = keep.tile([P, PASSES * N2 * PACK], F32)
+        b_float = keep.tile([P, N2 * PASSES * PACK], F32)
         nc.scalar.copy(out=b_float[:], in_=b_turned[:])
-        b_float_view = b_float[:].rearrange("p (g j t) -> p g j t", g=PASSES, t=PACK)
+        b_float_view = b_float[:].rearrange("p (j g t) -> p j g t", g=PASSES, t=PACK)
 
         c_codes = keep.tile([P, PASSES * N3], U32, align_bytes=64)
         c_scales = keep.tile([P, PASSES * N3], U8, align_bytes=64)
 
-        def multiply_on_vector(n, g):
+        def multiply_on_vector(n):
             j_rows = slice(n * J_GROUP, (n + 1) * J_GROUP)
-            shape = [P, J_GROUP, N1, PACK]
-            product = work.tile([P, GROUP_WORDS * PACK], BF16, align_bytes=64, name="product%d" % g)
+            shape = [P, J_GROUP, PASSES, N1, PACK]
+            product = products.tile([P, GROUP_COLS], BF16, align_bytes=64)
             nc.vector.tensor_tensor(
-                out=product[:].rearrange("p (j i t) -> p j i t", j=J_GROUP, t=PACK),
-                in0=a_view[:, g, :, :].unsqueeze(1).to_broadcast(shape),
-                in1=b_view[:, g, j_rows, :].unsqueeze(2).to_broadcast(shape),
+                out=product[:].rearrange("p (j g i t) -> p j g i t", j=J_GROUP, g=PASSES, t=PACK),
+                in0=a_view.unsqueeze(1).to_broadcast(shape),
+                in1=b_view[:, j_rows, :, :].unsqueeze(3).to_broadcast(shape),
                 op=mybir.AluOpType.mult,
             )
             return product
 
-        def multiply_on_scalar(n, g):
-            planes = scalar_work.tile([P, J_GROUP, PACK, N1], BF16)
+        def multiply_on_scalar(n):
+            planes = scalar_work.tile([P, J_GROUP * PASSES, PACK, N1], BF16)
             for j in range(J_GROUP):
-                for t in range(PACK):
-                    nc.scalar.activation(
-                        out=planes[:, j, t, :],
-                        in_=a_view[:, g, :, t],
-                        func=mybir.ActivationFunctionType.Copy,
-                        scale=b_float_view[:, g, n * J_GROUP + j, t : t + 1],
-                    )
-            product = scalar_work.tile(
-                [P, GROUP_WORDS * PACK], BF16, align_bytes=64, name="scalar_product%d" % g
-            )
+                for g in range(PASSES):
+                    for t in range(PACK):
+                        nc.scalar.activation(
+                            out=planes[:, j * PASSES + g, t, :],
+                            in_=a_view[:, g, :, t],
+                            func=mybir.ActivationFunctionType.Copy,
+                            scale=b_float_view[:, n * J_GROUP + j, g, t : t + 1],
+                        )
+            scalar_product = scalar_work.tile([P, GROUP_COLS], BF16, align_bytes=64)
             nc.scalar.copy(
-                out=product[:].rearrange("p (j i t) -> p j i t", j=J_GROUP, t=PACK),
-                in_=planes[:].rearrange("p j t i -> p j i t"),
+                out=scalar_product[:].rearrange("p (s i t) -> p s i t", s=J_GROUP * PASSES, t=PACK),
+                in_=planes[:].rearrange("p s t i -> p s i t"),
             )
-            return product
+            return scalar_product
 
-        def multiply_and_quantise(n):
-            multiply = multiply_on_scalar if n % SCALAR_EVERY == SCALAR_EVERY - 1 else multiply_on_vector
-            products = [multiply(n, g) for g in range(PASSES)]
-            codes = work.tile([P, PASSES, GROUP_WORDS], U32, align_bytes=64)
-            scales = work.tile([P, PASSES, GROUP_WORDS], U8, align_bytes=64)
-            for g in range(PASSES):
-                nc.vector.quantize_mx(
-                    out=codes[:, g, :].bitcast(FP8X4), scales=scales[:, g, :], in_=products[g][:]
-                )
+        def quantise(product):
+            codes = work.tile([P, GROUP_WORDS], U32, align_bytes=64)
+            scales = work.tile([P, GROUP_WORDS], U8, align_bytes=64)
+            nc.vector.quantize_mx(out=codes[:].bitcast(FP8X4), scales=scales[:], in_=product[:])
             return codes, scales
 
         def contract(codes, scales):
             sums = sums_psum.tile([P, J_GROUP, N3], F32)
             for j in range(J_GROUP):
-                i_cols = slice(j * N1, (j + 1) * N1)
                 for g in range(PASSES):
+                    i_cols = slice((j * PASSES + g) * N1, (j * PASSES + g + 1) * N1)
                     k_cols = slice(g * N3, (g + 1) * N3)
                     nc.tensor.matmul_mx(
                         out=sums[:, j, :],
-                        lhsT=codes[:, g, i_cols].bitcast(FP8X4),
-                        lhsT_scale=scales[:, g, i_cols],
+                        lhsT=codes[:, i_cols].bitcast(FP8X4),
+                        lhsT_scale=scales[:, i_cols],
                         rhs=c_codes[:, k_cols].bitcast(FP8X4),
                         rhs_scale=c_scales[:, k_cols],
                         start=(g == 0),
@@ -153,13 +154,26 @@ def tile_recon_loss_pa_t_kernel(tc, X, A, B, C, out):
             )
             nc.sync.dma_start(out=out_rows[:, n * width : (n + 1) * width], in_=residual[:])
 
+        scalar_groups = [n for n in range(GROUPS) if n % SCALAR_EVERY == SCALAR_EVERY - 1]
+        vector_groups = [n for n in range(GROUPS) if n % SCALAR_EVERY != SCALAR_EVERY - 1]
+        ready = {}
+
+        def start(groups, multiply, place):
+            if place < len(groups):
+                ready[groups[place]] = multiply(groups[place])
+
+        for place in range(2):
+            start(scalar_groups, multiply_on_scalar, place)
+            start(vector_groups, multiply_on_vector, place)
+        nc.vector.quantize_mx(out=c_codes[:].bitcast(FP8X4), scales=c_scales[:], in_=c_turned[:])
+
         waiting = None
         for n in range(GROUPS):
-            codes, scales = multiply_and_quantise(n)
-            if n == 0:
-                nc.vector.quantize_mx(
-                    out=c_codes[:].bitcast(FP8X4), scales=c_scales[:], in_=c_turned[:]
-                )
+            codes, scales = quantise(ready.pop(n))
+            if n in scalar_groups:
+                start(scalar_groups, multiply_on_scalar, scalar_groups.index(n) + 2)
+            else:
+                start(vector_groups, multiply_on_vector, vector_groups.index(n) + 2)
             sums = contract(codes, scales)
             if waiting is not None:
                 subtract_and_store(n - 1, waiting)

@@ -43,7 +43,7 @@ def tile_recon_loss_pa_t_kernel(tc, X, A, B, C, out):
     out_rows = out.rearrange("i j k -> i (j k)")
 
     with tc.tile_pool(name="keep", bufs=1) as keep, tc.tile_pool(name="work", bufs=3) as work, tc.tile_pool(
-        name="products", bufs=2
+        name="products", bufs=3
     ) as products, tc.tile_pool(name="scalar_work", bufs=2) as scalar_work, tc.psum_pool(
         name="turn", bufs=2
     ) as turn_psum, tc.psum_pool(name="sums", bufs=3) as sums_psum, tc.manual_schedule():

@@ -46,7 +46,7 @@ def tile_recon_loss_pa_t_kernel(tc, X, A, B, C, out):
         name="products", bufs=3
     ) as products, tc.tile_pool(name="scalar_work", bufs=2) as scalar_work, tc.psum_pool(
         name="turn", bufs=2
-    ) as turn_psum, tc.psum_pool(name="sums", bufs=3) as sums_psum, tc.manual_schedule():
+    ) as turn_psum, tc.psum_pool(name="a_psum", bufs=1) as a_psum, tc.psum_pool(name="sums", bufs=3) as sums_psum, tc.manual_schedule():
         a_raw = keep.tile([P, R], BF16)
         b_raw = keep.tile([P, R], BF16)
         c_raw = keep.tile([P, R], BF16)
@@ -81,6 +81,14 @@ def tile_recon_loss_pa_t_kernel(tc, X, A, B, C, out):
         a_view = a_turned[:].rearrange("p (g i t) -> p g i t", g=PASSES, t=PACK)
         b_view = b_turned[:].rearrange("p (j g t) -> p j g t", g=PASSES, t=PACK)
 
+        ident_bf = keep.tile([P, P], BF16)
+        make_identity(nc, ident_bf[:])
+        a_bank = a_psum.tile([P, PASSES * N1 * PACK], BF16)
+        for g in range(PASSES):
+            g_cols = slice(g * N1 * PACK, (g + 1) * N1 * PACK)
+            nc.tensor.matmul(out=a_bank[:, g_cols], lhsT=ident_bf[:], rhs=a_turned[:, g_cols], start=True, stop=True)
+        a_bank_view = a_bank[:].rearrange("p (g i t) -> p g i t", g=PASSES, t=PACK)
+
         b_float = keep.tile([P, N2 * PASSES * PACK], F32)
         nc.scalar.copy(out=b_float[:], in_=b_turned[:])
         b_float_view = b_float[:].rearrange("p (j g t) -> p j g t", g=PASSES, t=PACK)
@@ -94,7 +102,7 @@ def tile_recon_loss_pa_t_kernel(tc, X, A, B, C, out):
             product = products.tile([P, GROUP_COLS], BF16, align_bytes=64)
             nc.vector.tensor_tensor(
                 out=product[:].rearrange("p (j g i t) -> p j g i t", j=J_GROUP, g=PASSES, t=PACK),
-                in0=a_view.unsqueeze(1).to_broadcast(shape),
+                in0=a_bank_view.unsqueeze(1).to_broadcast(shape),
                 in1=b_view[:, j_rows, :, :].unsqueeze(3).to_broadcast(shape),
                 op=mybir.AluOpType.mult,
             )

@@ -15,24 +15,33 @@ N2 = 128
 N3 = 128
 R = 1024
 PASSES = R // K_PASS
-PAIRS = PACK // 2
+HALVES = PACK // 2
 
 J_GROUP = 4
 GROUPS = N2 // J_GROUP
-GROUP_WORDS = J_GROUP * PASSES * N1
-GROUP_COLS = GROUP_WORDS * PACK
-SCALAR_EVERY = 4
+J_COLS = PASSES * N1 * PACK
+GROUP_COLS = J_GROUP * J_COLS
+GROUP_WORDS = GROUP_COLS // PACK
+GROUP_OUT = J_GROUP * N3
+STEPS = GROUPS // 2
+VECTOR_TAIL_STEPS = 2
+SLOTS = 8
+SLOT_BYTES = GROUP_COLS * 2
 X_CHUNK_J = 16
 X_CHUNKS = N2 // X_CHUNK_J
 
 FLOPS = 2 * N1 * N2 * N3 * R
 
 
+def scalar_helps(n):
+    return n % 4 != 0
+
+
 def turn_factor(nc, psum, ident, raw, copy, turned_words):
-    words = raw[:].bitcast(F32).rearrange("row (g p u) -> row g u p", g=PASSES, u=PAIRS)
-    flipped = psum.tile([P, PASSES, PAIRS, P], F32)
+    words = raw[:].bitcast(F32).rearrange("row (g p u) -> row g u p", g=PASSES, u=HALVES)
+    flipped = psum.tile([P, PASSES, HALVES, P], F32)
     for g in range(PASSES):
-        for u in range(PAIRS):
+        for u in range(HALVES):
             nc.tensor.transpose(flipped[:, g, u, :], words[:, g, u, :], ident[:])
     copy(out=turned_words, in_=flipped[:].rearrange("p g u row -> p g row u"))
 
@@ -42,11 +51,13 @@ def tile_recon_loss_pa_t_kernel(tc, X, A, B, C, out):
     x_rows = X.rearrange("i j k -> i (j k)")
     out_rows = out.rearrange("i j k -> i (j k)")
 
-    with tc.tile_pool(name="keep", bufs=1) as keep, tc.tile_pool(name="work", bufs=3) as work, tc.tile_pool(
-        name="products", bufs=3
-    ) as products, tc.tile_pool(name="scalar_work", bufs=2) as scalar_work, tc.psum_pool(
+    with tc.tile_pool(name="keep", bufs=1) as keep, tc.tile_pool(name="work", bufs=4) as work, tc.tile_pool(
+        name="products", bufs=1
+    ) as products, tc.tile_pool(name="scalar_work", bufs=3) as scalar_work, tc.psum_pool(
         name="turn", bufs=2
-    ) as turn_psum, tc.psum_pool(name="a_psum", bufs=1) as a_psum, tc.psum_pool(name="sums", bufs=3) as sums_psum, tc.manual_schedule():
+    ) as turn_psum, tc.psum_pool(name="a_psum", bufs=1) as a_psum, tc.psum_pool(
+        name="sums", bufs=5
+    ) as sums_psum, tc.manual_schedule():
         a_raw = keep.tile([P, R], BF16)
         b_raw = keep.tile([P, R], BF16)
         c_raw = keep.tile([P, R], BF16)
@@ -62,27 +73,27 @@ def tile_recon_loss_pa_t_kernel(tc, X, A, B, C, out):
 
         ident = keep.tile([P, P], F32)
         make_identity(nc, ident[:])
+        ident_bf = keep.tile([P, P], BF16)
+        make_identity(nc, ident_bf[:])
 
         a_turned = keep.tile([P, PASSES * N1 * PACK], BF16)
         b_turned = keep.tile([P, N2 * PASSES * PACK], BF16)
         c_turned = keep.tile([P, PASSES * N3 * PACK], BF16, align_bytes=64)
         turn_factor(
             nc, turn_psum, ident, a_raw, nc.vector.tensor_copy,
-            a_turned[:].bitcast(F32).rearrange("p (g row u) -> p g row u", g=PASSES, u=PAIRS),
+            a_turned[:].bitcast(F32).rearrange("p (g row u) -> p g row u", g=PASSES, u=HALVES),
         )
         turn_factor(
             nc, turn_psum, ident, b_raw, nc.scalar.copy,
-            b_turned[:].bitcast(F32).rearrange("p (row g u) -> p g row u", g=PASSES, u=PAIRS),
+            b_turned[:].bitcast(F32).rearrange("p (row g u) -> p g row u", g=PASSES, u=HALVES),
         )
         turn_factor(
             nc, turn_psum, ident, c_raw, nc.scalar.copy,
-            c_turned[:].bitcast(F32).rearrange("p (g row u) -> p g row u", g=PASSES, u=PAIRS),
+            c_turned[:].bitcast(F32).rearrange("p (g row u) -> p g row u", g=PASSES, u=HALVES),
         )
         a_view = a_turned[:].rearrange("p (g i t) -> p g i t", g=PASSES, t=PACK)
         b_view = b_turned[:].rearrange("p (j g t) -> p j g t", g=PASSES, t=PACK)
 
-        ident_bf = keep.tile([P, P], BF16)
-        make_identity(nc, ident_bf[:])
         a_bank = a_psum.tile([P, PASSES * N1 * PACK], BF16)
         for g in range(PASSES):
             g_cols = slice(g * N1 * PACK, (g + 1) * N1 * PACK)
@@ -96,40 +107,52 @@ def tile_recon_loss_pa_t_kernel(tc, X, A, B, C, out):
         c_codes = keep.tile([P, PASSES * N3], U32, align_bytes=64)
         c_scales = keep.tile([P, PASSES * N3], U8, align_bytes=64)
 
+        product_of = {}
+
+        def new_product(n):
+            slot = n % SLOTS
+            product_of[n] = products.tile(
+                [P, GROUP_COLS], BF16, name="product%d" % slot, tag="product%d" % slot,
+                offset=slot * SLOT_BYTES, align_bytes=64,
+            )
+
         def multiply_on_vector(n):
-            j_rows = slice(n * J_GROUP, (n + 1) * J_GROUP)
-            shape = [P, J_GROUP, PASSES, N1, PACK]
-            product = products.tile([P, GROUP_COLS], BF16, align_bytes=64)
+            j_count = J_GROUP - 1 if scalar_helps(n) else J_GROUP
+            j_rows = slice(n * J_GROUP, n * J_GROUP + j_count)
+            shape = [P, j_count, PASSES, N1, PACK]
             nc.vector.tensor_tensor(
-                out=product[:].rearrange("p (j g i t) -> p j g i t", j=J_GROUP, g=PASSES, t=PACK),
+                out=product_of[n][:, 0 : j_count * J_COLS].rearrange(
+                    "p (j g i t) -> p j g i t", j=j_count, g=PASSES, t=PACK
+                ),
                 in0=a_bank_view.unsqueeze(1).to_broadcast(shape),
                 in1=b_view[:, j_rows, :, :].unsqueeze(3).to_broadcast(shape),
                 op=mybir.AluOpType.mult,
             )
-            return product
 
         def multiply_on_scalar(n):
-            planes = scalar_work.tile([P, J_GROUP * PASSES, PACK, N1], BF16)
-            for j in range(J_GROUP):
-                for g in range(PASSES):
-                    for t in range(PACK):
-                        nc.scalar.activation(
-                            out=planes[:, j * PASSES + g, t, :],
-                            in_=a_view[:, g, :, t],
-                            func=mybir.ActivationFunctionType.Copy,
-                            scale=b_float_view[:, n * J_GROUP + j, g, t : t + 1],
-                        )
-            scalar_product = scalar_work.tile([P, GROUP_COLS], BF16, align_bytes=64)
+            if not scalar_helps(n):
+                return
+            j = n * J_GROUP + J_GROUP - 1
+            planes = scalar_work.tile([P, PASSES, PACK, N1], BF16)
+            for g in range(PASSES):
+                for t in range(PACK):
+                    nc.scalar.activation(
+                        out=planes[:, g, t, :],
+                        in_=a_view[:, g, :, t],
+                        func=mybir.ActivationFunctionType.Copy,
+                        scale=b_float_view[:, j, g, t : t + 1],
+                    )
             nc.scalar.copy(
-                out=scalar_product[:].rearrange("p (s i t) -> p s i t", s=J_GROUP * PASSES, t=PACK),
-                in_=planes[:].rearrange("p s t i -> p s i t"),
+                out=product_of[n][:, (J_GROUP - 1) * J_COLS : GROUP_COLS].rearrange(
+                    "p (g i t) -> p g i t", g=PASSES, t=PACK
+                ),
+                in_=planes[:].rearrange("p g t i -> p g i t"),
             )
-            return scalar_product
 
-        def quantise(product):
+        def quantise(n):
             codes = work.tile([P, GROUP_WORDS], U32, align_bytes=64)
             scales = work.tile([P, GROUP_WORDS], U8, align_bytes=64)
-            nc.vector.quantize_mx(out=codes[:].bitcast(FP8X4), scales=scales[:], in_=product[:])
+            nc.vector.quantize_mx(out=codes[:].bitcast(FP8X4), scales=scales[:], in_=product_of[n][:])
             return codes, scales
 
         def contract(codes, scales):
@@ -149,41 +172,67 @@ def tile_recon_loss_pa_t_kernel(tc, X, A, B, C, out):
                     )
             return sums
 
-        def subtract_and_store(n, sums):
-            width = J_GROUP * N3
-            first = (n * J_GROUP % X_CHUNK_J) * N3
-            x_part = x_chunks[n * J_GROUP // X_CHUNK_J][:, first : first + width]
-            residual = work.tile([P, width], F32)
+        def x_part(first_group, groups):
+            first = (first_group * J_GROUP % X_CHUNK_J) * N3
+            return x_chunks[first_group * J_GROUP // X_CHUNK_J][:, first : first + groups * GROUP_OUT]
+
+        def subtract_on_vector(n, sums):
+            residual = work.tile([P, GROUP_OUT], F32)
             nc.vector.tensor_tensor(
                 out=residual[:],
                 in0=sums[:].rearrange("p j k -> p (j k)"),
-                in1=x_part,
+                in1=x_part(n, 1),
                 op=mybir.AluOpType.subtract,
             )
-            nc.sync.dma_start(out=out_rows[:, n * width : (n + 1) * width], in_=residual[:])
+            nc.sync.dma_start(out=out_rows[:, n * GROUP_OUT : (n + 1) * GROUP_OUT], in_=residual[:])
 
-        scalar_groups = [n for n in range(GROUPS) if n % SCALAR_EVERY == SCALAR_EVERY - 1]
-        vector_groups = [n for n in range(GROUPS) if n % SCALAR_EVERY != SCALAR_EVERY - 1]
-        ready = {}
+        def empty_on_scalar(pair_sums):
+            emptied = scalar_work.tile([P, 2 * GROUP_OUT], F32)
+            for half in range(2):
+                nc.scalar.copy(
+                    out=emptied[:, half * GROUP_OUT : (half + 1) * GROUP_OUT],
+                    in_=pair_sums[half][:].rearrange("p j k -> p (j k)"),
+                )
+            return emptied
 
-        def start(groups, multiply, place):
-            if place < len(groups):
-                ready[groups[place]] = multiply(groups[place])
+        def subtract_on_gpsimd(step, emptied, slot):
+            residual_pair = products.tile(
+                [P, 2 * GROUP_OUT], F32, name="residual%d" % slot, tag="residual%d" % slot,
+                offset=slot * SLOT_BYTES, align_bytes=64,
+            )
+            nc.gpsimd.tensor_tensor(
+                out=residual_pair[:], in0=emptied[:], in1=x_part(2 * step, 2), op=mybir.AluOpType.subtract
+            )
+            cols = slice(2 * step * GROUP_OUT, (2 * step + 2) * GROUP_OUT)
+            nc.sync.dma_start(out=out_rows[:, cols], in_=residual_pair[:])
 
-        for place in range(2):
-            start(scalar_groups, multiply_on_scalar, place)
-            start(vector_groups, multiply_on_vector, place)
+        for n in range(6):
+            new_product(n)
+        multiply_on_vector(0)
+        multiply_on_vector(1)
+        for n in range(6):
+            multiply_on_scalar(n)
         nc.vector.quantize_mx(out=c_codes[:].bitcast(FP8X4), scales=c_scales[:], in_=c_turned[:])
 
-        waiting = None
-        for n in range(GROUPS):
-            codes, scales = quantise(ready.pop(n))
-            if n in scalar_groups:
-                start(scalar_groups, multiply_on_scalar, scalar_groups.index(n) + 2)
+        emptied_before = None
+        kept_sums = []
+        for step in range(STEPS):
+            pair = (2 * step, 2 * step + 1)
+            quantised = [quantise(n) for n in pair]
+            pair_sums = [contract(codes, scales) for codes, scales in quantised]
+            if emptied_before is not None:
+                subtract_on_gpsimd(step - 1, emptied_before, pair[1] % SLOTS)
+                emptied_before = None
+            for n in pair:
+                if n + 2 < GROUPS:
+                    multiply_on_vector(n + 2)
+            if step < STEPS - VECTOR_TAIL_STEPS:
+                emptied_before = empty_on_scalar(pair_sums)
             else:
-                start(vector_groups, multiply_on_vector, vector_groups.index(n) + 2)
-            sums = contract(codes, scales)
-            if waiting is not None:
-                subtract_and_store(n - 1, waiting)
-            waiting = sums
-        subtract_and_store(GROUPS - 1, waiting)
+                kept_sums.extend(zip(pair, pair_sums))
+            for n in pair:
+                if n + 6 < GROUPS:
+                    new_product(n + 6)
+                    multiply_on_scalar(n + 6)
+        for n, sums in kept_sums:
+            subtract_on_vector(n, sums)

@@ -34,16 +34,23 @@ FLOPS = 2 * N1 * N2 * N3 * R
 
 
 def scalar_helps(n):
-    return n % 4 != 0
+    return n % 8 != 0
 
 
-def turn_factor(nc, psum, ident, raw, copy, turned_words):
+def flip_words(nc, ident, raw, flipped):
     words = raw[:].bitcast(F32).rearrange("row (g p u) -> row g u p", g=PASSES, u=HALVES)
-    flipped = psum.tile([P, PASSES, HALVES, P], F32)
     for g in range(PASSES):
         for u in range(HALVES):
             nc.tensor.transpose(flipped[:, g, u, :], words[:, g, u, :], ident[:])
-    copy(out=turned_words, in_=flipped[:].rearrange("p g u row -> p g row u"))
+
+
+def turn_factor(nc, psum, ident, raw, copy, turned, order):
+    flipped = psum.tile([P, PASSES, HALVES, P], F32)
+    flip_words(nc, ident, raw, flipped[:])
+    copy(
+        out=turned[:].bitcast(F32).rearrange("p (%s) -> p %s" % (order, order), g=PASSES, u=HALVES),
+        in_=flipped[:].rearrange("p g u row -> p %s" % order),
+    )
 
 
 def tile_recon_loss_pa_t_kernel(tc, X, A, B, C, out):
@@ -61,8 +68,8 @@ def tile_recon_loss_pa_t_kernel(tc, X, A, B, C, out):
         a_raw = keep.tile([P, R], BF16)
         b_raw = keep.tile([P, R], BF16)
         c_raw = keep.tile([P, R], BF16)
+        nc.sync.dma_start(out=b_raw[:], in_=B[:, :])
         nc.sync.dma_start(out=a_raw[:], in_=A[:, :])
-        nc.scalar.dma_start(out=b_raw[:], in_=B[:, :])
         nc.sync.dma_start(out=c_raw[:], in_=C[:, :])
         x_chunks = []
         for c in range(X_CHUNKS):
@@ -73,32 +80,21 @@ def tile_recon_loss_pa_t_kernel(tc, X, A, B, C, out):
 
         ident = keep.tile([P, P], F32)
         make_identity(nc, ident[:])
-        ident_bf = keep.tile([P, P], BF16)
-        make_identity(nc, ident_bf[:])
 
         a_turned = keep.tile([P, PASSES * N1 * PACK], BF16)
         b_turned = keep.tile([P, N2 * PASSES * PACK], BF16)
         c_turned = keep.tile([P, PASSES * N3 * PACK], BF16, align_bytes=64)
-        turn_factor(
-            nc, turn_psum, ident, a_raw, nc.vector.tensor_copy,
-            a_turned[:].bitcast(F32).rearrange("p (g row u) -> p g row u", g=PASSES, u=HALVES),
-        )
-        turn_factor(
-            nc, turn_psum, ident, b_raw, nc.scalar.copy,
-            b_turned[:].bitcast(F32).rearrange("p (row g u) -> p g row u", g=PASSES, u=HALVES),
-        )
-        turn_factor(
-            nc, turn_psum, ident, c_raw, nc.scalar.copy,
-            c_turned[:].bitcast(F32).rearrange("p (g row u) -> p g row u", g=PASSES, u=HALVES),
-        )
+        turn_factor(nc, turn_psum, ident, b_raw, nc.vector.tensor_copy, b_turned, "row g u")
+        a_bank = a_psum.tile([P, PASSES, N1, HALVES], F32)
+        flip_words(nc, ident, a_raw, a_bank[:].rearrange("p g i u -> p g u i"))
+        turn_factor(nc, turn_psum, ident, a_raw, nc.scalar.copy, a_turned, "g row u")
+        turn_factor(nc, turn_psum, ident, c_raw, nc.scalar.copy, c_turned, "g row u")
         a_view = a_turned[:].rearrange("p (g i t) -> p g i t", g=PASSES, t=PACK)
         b_view = b_turned[:].rearrange("p (j g t) -> p j g t", g=PASSES, t=PACK)
 
-        a_bank = a_psum.tile([P, PASSES * N1 * PACK], BF16)
-        for g in range(PASSES):
-            g_cols = slice(g * N1 * PACK, (g + 1) * N1 * PACK)
-            nc.tensor.matmul(out=a_bank[:, g_cols], lhsT=ident_bf[:], rhs=a_turned[:, g_cols], start=True, stop=True)
-        a_bank_view = a_bank[:].rearrange("p (g i t) -> p g i t", g=PASSES, t=PACK)
+        a_bank_view = (
+            a_bank[:].rearrange("p g i u -> p (g i u)").bitcast(BF16).rearrange("p (g i t) -> p g i t", g=PASSES, t=PACK)
+        )
 
         b_float = keep.tile([P, N2 * PASSES * PACK], F32)
         nc.scalar.copy(out=b_float[:], in_=b_turned[:])

@@ -44,9 +44,7 @@ def flip_words(nc, ident, raw, flipped):
             nc.tensor.transpose(flipped[:, g, u, :], words[:, g, u, :], ident[:])
 
 
-def turn_factor(nc, psum, ident, raw, copy, turned, order):
-    flipped = psum.tile([P, PASSES, HALVES, P], F32)
-    flip_words(nc, ident, raw, flipped[:])
+def copy_flipped(copy, flipped, turned, order):
     copy(
         out=turned[:].bitcast(F32).rearrange("p (%s) -> p %s" % (order, order), g=PASSES, u=HALVES),
         in_=flipped[:].rearrange("p g u row -> p %s" % order),
@@ -84,11 +82,15 @@ def tile_recon_loss_pa_t_kernel(tc, X, A, B, C, out):
         a_turned = keep.tile([P, PASSES * N1 * PACK], BF16)
         b_turned = keep.tile([P, N2 * PASSES * PACK], BF16)
         c_turned = keep.tile([P, PASSES * N3 * PACK], BF16, align_bytes=64)
-        turn_factor(nc, turn_psum, ident, b_raw, nc.vector.tensor_copy, b_turned, "row g u")
+        b_flipped = turn_psum.tile([P, PASSES, HALVES, P], F32, tag="flipped")
+        flip_words(nc, ident, b_raw, b_flipped[:])
+        copy_flipped(nc.vector.tensor_copy, b_flipped, b_turned, "row g u")
         a_bank = a_psum.tile([P, PASSES, N1, HALVES], F32)
         flip_words(nc, ident, a_raw, a_bank[:].rearrange("p g i u -> p g u i"))
-        turn_factor(nc, turn_psum, ident, a_raw, nc.scalar.copy, a_turned, "g row u")
-        turn_factor(nc, turn_psum, ident, c_raw, nc.scalar.copy, c_turned, "g row u")
+        a_flipped = turn_psum.tile([P, PASSES, HALVES, P], F32, tag="flipped")
+        flip_words(nc, ident, a_raw, a_flipped[:])
+        c_flipped = turn_psum.tile([P, PASSES, HALVES, P], F32, tag="flipped")
+        flip_words(nc, ident, c_raw, c_flipped[:])
         a_view = a_turned[:].rearrange("p (g i t) -> p g i t", g=PASSES, t=PACK)
         b_view = b_turned[:].rearrange("p (j g t) -> p j g t", g=PASSES, t=PACK)
 
@@ -96,9 +98,12 @@ def tile_recon_loss_pa_t_kernel(tc, X, A, B, C, out):
             a_bank[:].rearrange("p g i u -> p (g i u)").bitcast(BF16).rearrange("p (g i t) -> p g i t", g=PASSES, t=PACK)
         )
 
-        b_float = keep.tile([P, N2 * PASSES * PACK], F32)
-        nc.scalar.copy(out=b_float[:], in_=b_turned[:])
-        b_float_view = b_float[:].rearrange("p (j g t) -> p j g t", g=PASSES, t=PACK)
+        b_last = keep.tile([P, GROUPS, PASSES, PACK], F32)
+        nc.scalar.copy(
+            out=b_last[:],
+            in_=b_turned[:].rearrange("p (n j g t) -> p n j g t", j=J_GROUP, g=PASSES, t=PACK)[:, :, J_GROUP - 1, :, :],
+        )
+        copy_flipped(nc.scalar.copy, a_flipped, a_turned, "g row u")
 
         c_codes = keep.tile([P, PASSES * N3], U32, align_bytes=64)
         c_scales = keep.tile([P, PASSES * N3], U8, align_bytes=64)
@@ -125,10 +130,20 @@ def tile_recon_loss_pa_t_kernel(tc, X, A, B, C, out):
                 op=mybir.AluOpType.mult,
             )
 
+        planes_waiting = []
+
+        def regroup_on_scalar():
+            n, planes = planes_waiting.pop(0)
+            nc.scalar.copy(
+                out=product_of[n][:, (J_GROUP - 1) * J_COLS : GROUP_COLS].rearrange(
+                    "p (g i t) -> p g i t", g=PASSES, t=PACK
+                ),
+                in_=planes[:].rearrange("p g t i -> p g i t"),
+            )
+
         def multiply_on_scalar(n):
             if not scalar_helps(n):
                 return
-            j = n * J_GROUP + J_GROUP - 1
             planes = scalar_work.tile([P, PASSES, PACK, N1], BF16)
             for g in range(PASSES):
                 for t in range(PACK):
@@ -136,14 +151,11 @@ def tile_recon_loss_pa_t_kernel(tc, X, A, B, C, out):
                         out=planes[:, g, t, :],
                         in_=a_view[:, g, :, t],
                         func=mybir.ActivationFunctionType.Copy,
-                        scale=b_float_view[:, j, g, t : t + 1],
+                        scale=b_last[:, n, g, t : t + 1],
                     )
-            nc.scalar.copy(
-                out=product_of[n][:, (J_GROUP - 1) * J_COLS : GROUP_COLS].rearrange(
-                    "p (g i t) -> p g i t", g=PASSES, t=PACK
-                ),
-                in_=planes[:].rearrange("p g t i -> p g i t"),
-            )
+            planes_waiting.append((n, planes))
+            if len(planes_waiting) > 1:
+                regroup_on_scalar()
 
         def quantise(n):
             codes = work.tile([P, GROUP_WORDS], U32, align_bytes=64)
@@ -206,7 +218,10 @@ def tile_recon_loss_pa_t_kernel(tc, X, A, B, C, out):
             new_product(n)
         multiply_on_vector(0)
         multiply_on_vector(1)
-        for n in range(6):
+        multiply_on_scalar(1)
+        copy_flipped(nc.scalar.copy, c_flipped, c_turned, "g row u")
+        regroup_on_scalar()
+        for n in range(2, 6):
             multiply_on_scalar(n)
         nc.vector.quantize_mx(out=c_codes[:].bitcast(FP8X4), scales=c_scales[:], in_=c_turned[:])
 
@@ -230,5 +245,7 @@ def tile_recon_loss_pa_t_kernel(tc, X, A, B, C, out):
                 if n + 6 < GROUPS:
                     new_product(n + 6)
                     multiply_on_scalar(n + 6)
+                if n + 6 == GROUPS - 1:
+                    regroup_on_scalar()
         for n, sums in kept_sums:
             subtract_on_vector(n, sums)

@@ -34,7 +34,11 @@ FLOPS = 2 * N1 * N2 * N3 * R
 
 
 def scalar_helps(n):
-    return n % 8 != 0
+    return n > 0
+
+
+def tensor_regroups(n):
+    return n % 3 == 1
 
 
 def flip_words(nc, ident, raw, flipped):
@@ -78,6 +82,8 @@ def tile_recon_loss_pa_t_kernel(tc, X, A, B, C, out):
 
         ident = keep.tile([P, P], F32)
         make_identity(nc, ident[:])
+        ident_bf = keep.tile([P, P], BF16)
+        make_identity(nc, ident_bf[:])
 
         a_turned = keep.tile([P, PASSES * N1 * PACK], BF16)
         b_turned = keep.tile([P, N2 * PASSES * PACK], BF16)
@@ -134,12 +140,23 @@ def tile_recon_loss_pa_t_kernel(tc, X, A, B, C, out):
 
         def regroup_on_scalar():
             n, planes = planes_waiting.pop(0)
-            nc.scalar.copy(
-                out=product_of[n][:, (J_GROUP - 1) * J_COLS : GROUP_COLS].rearrange(
-                    "p (g i t) -> p g i t", g=PASSES, t=PACK
-                ),
-                in_=planes[:].rearrange("p g t i -> p g i t"),
-            )
+            last_j = product_of[n][:, (J_GROUP - 1) * J_COLS : GROUP_COLS]
+            if tensor_regroups(n):
+                regrouped = turn_psum.tile([P, PASSES, N1 * PACK], BF16, tag="flipped")
+                for g in range(PASSES):
+                    nc.tensor.matmul(
+                        out=regrouped[:, g, :],
+                        lhsT=ident_bf[:],
+                        rhs=planes[:, g, :, :].rearrange("p t i -> p i t"),
+                        start=True,
+                        stop=True,
+                    )
+                nc.scalar.copy(out=last_j, in_=regrouped[:].rearrange("p g c -> p (g c)"))
+            else:
+                nc.scalar.copy(
+                    out=last_j.rearrange("p (g i t) -> p g i t", g=PASSES, t=PACK),
+                    in_=planes[:].rearrange("p g t i -> p g i t"),
+                )
 
         def multiply_on_scalar(n):
             if not scalar_helps(n):

@@ -27,6 +27,7 @@ STEPS = GROUPS // 2
 VECTOR_TAIL_STEPS = 2
 SLOTS = 8
 SLOT_BYTES = GROUP_COLS * 2
+PLANES_BUFS = 5
 X_CHUNK_J = 16
 X_CHUNKS = N2 // X_CHUNK_J
 
@@ -138,19 +139,25 @@ def tile_recon_loss_pa_t_kernel(tc, X, A, B, C, out):
 
         planes_waiting = []
 
-        def regroup_on_scalar():
-            n, planes = planes_waiting.pop(0)
+        def regroup_on_tensor():
+            for entry in planes_waiting:
+                n, planes, regrouped = entry
+                if tensor_regroups(n) and regrouped is None:
+                    regrouped = turn_psum.tile([P, PASSES, N1 * PACK], BF16, tag="flipped")
+                    for g in range(PASSES):
+                        nc.tensor.matmul(
+                            out=regrouped[:, g, :],
+                            lhsT=ident_bf[:],
+                            rhs=planes[:, g, :, :].rearrange("p t i -> p i t"),
+                            start=True,
+                            stop=True,
+                        )
+                    entry[2] = regrouped
+
+        def finish_on_scalar():
+            n, planes, regrouped = planes_waiting.pop(0)
             last_j = product_of[n][:, (J_GROUP - 1) * J_COLS : GROUP_COLS]
             if tensor_regroups(n):
-                regrouped = turn_psum.tile([P, PASSES, N1 * PACK], BF16, tag="flipped")
-                for g in range(PASSES):
-                    nc.tensor.matmul(
-                        out=regrouped[:, g, :],
-                        lhsT=ident_bf[:],
-                        rhs=planes[:, g, :, :].rearrange("p t i -> p i t"),
-                        start=True,
-                        stop=True,
-                    )
                 nc.scalar.copy(out=last_j, in_=regrouped[:].rearrange("p g c -> p (g c)"))
             else:
                 nc.scalar.copy(
@@ -158,10 +165,10 @@ def tile_recon_loss_pa_t_kernel(tc, X, A, B, C, out):
                     in_=planes[:].rearrange("p g t i -> p g i t"),
                 )
 
-        def multiply_on_scalar(n):
+        def multiply_on_scalar(n, may_wait):
             if not scalar_helps(n):
                 return
-            planes = scalar_work.tile([P, PASSES, PACK, N1], BF16)
+            planes = scalar_work.tile([P, PASSES, PACK, N1], BF16, bufs=PLANES_BUFS)
             for g in range(PASSES):
                 for t in range(PACK):
                     nc.scalar.activation(
@@ -170,9 +177,9 @@ def tile_recon_loss_pa_t_kernel(tc, X, A, B, C, out):
                         func=mybir.ActivationFunctionType.Copy,
                         scale=b_last[:, n, g, t : t + 1],
                     )
-            planes_waiting.append((n, planes))
-            if len(planes_waiting) > 1:
-                regroup_on_scalar()
+            planes_waiting.append([n, planes, None])
+            if len(planes_waiting) > may_wait:
+                finish_on_scalar()
 
         def quantise(n):
             codes = work.tile([P, GROUP_WORDS], U32, align_bytes=64)
@@ -235,11 +242,13 @@ def tile_recon_loss_pa_t_kernel(tc, X, A, B, C, out):
             new_product(n)
         multiply_on_vector(0)
         multiply_on_vector(1)
-        multiply_on_scalar(1)
+        multiply_on_scalar(1, 1)
         copy_flipped(nc.scalar.copy, c_flipped, c_turned, "g row u")
-        regroup_on_scalar()
-        for n in range(2, 6):
-            multiply_on_scalar(n)
+        regroup_on_tensor()
+        finish_on_scalar()
+        for n in range(2, 5):
+            multiply_on_scalar(n, 1)
+        multiply_on_scalar(5, 2)
         nc.vector.quantize_mx(out=c_codes[:].bitcast(FP8X4), scales=c_scales[:], in_=c_turned[:])
 
         emptied_before = None
@@ -248,6 +257,7 @@ def tile_recon_loss_pa_t_kernel(tc, X, A, B, C, out):
             pair = (2 * step, 2 * step + 1)
             quantised = [quantise(n) for n in pair]
             pair_sums = [contract(codes, scales) for codes, scales in quantised]
+            regroup_on_tensor()
             if emptied_before is not None:
                 subtract_on_gpsimd(step - 1, emptied_before, pair[1] % SLOTS)
                 emptied_before = None
@@ -261,8 +271,8 @@ def tile_recon_loss_pa_t_kernel(tc, X, A, B, C, out):
             for n in pair:
                 if n + 6 < GROUPS:
                     new_product(n + 6)
-                    multiply_on_scalar(n + 6)
-                if n + 6 == GROUPS - 1:
-                    regroup_on_scalar()
+                    multiply_on_scalar(n + 6, 2)
+                elif planes_waiting:
+                    finish_on_scalar()
         for n, sums in kept_sums:
             subtract_on_vector(n, sums)

@@ -228,10 +228,7 @@ def tile_recon_loss_pa_t_kernel(tc, X, A, B, C, out):
             return emptied
 
         def subtract_on_gpsimd(step, emptied, slot):
-            residual_pair = products.tile(
-                [P, 2 * GROUP_OUT], F32, name="residual%d" % slot, tag="residual%d" % slot,
-                offset=slot * SLOT_BYTES, align_bytes=64,
-            )
+            residual_pair = scalar_work.tile([P, 2 * GROUP_OUT], F32)
             nc.gpsimd.tensor_tensor(
                 out=residual_pair[:], in0=emptied[:], in1=x_part(2 * step, 2), op=mybir.AluOpType.subtract
             )

@@ -34,12 +34,22 @@ X_CHUNKS = N2 // X_CHUNK_J
 FLOPS = 2 * N1 * N2 * N3 * R
 
 
-def scalar_helps(n):
-    return n > 0
+HEAD_ROWS = 12
+EXTRA_GROUPS = 2
 
 
-def tensor_regroups(n):
-    return n % 3 == 1
+def scalar_j(n):
+    if n < 2:
+        return 0
+    return 2 if n >= GROUPS - EXTRA_GROUPS else 1
+
+
+def gpsimd_j(n):
+    return 1 if n == 1 else 0
+
+
+def tensor_regroups(n, j):
+    return n % 3 == 1 and j == J_GROUP - 1
 
 
 def flip_words(nc, ident, raw, flipped):
@@ -51,8 +61,8 @@ def flip_words(nc, ident, raw, flipped):
 
 def copy_flipped(copy, flipped, turned, order):
     copy(
-        out=turned[:].bitcast(F32).rearrange("p (%s) -> p %s" % (order, order), g=PASSES, u=HALVES),
-        in_=flipped[:].rearrange("p g u row -> p %s" % order),
+        out=turned.bitcast(F32).rearrange("p (%s) -> p %s" % (order, order), g=PASSES, u=HALVES),
+        in_=flipped.rearrange("p g u row -> p %s" % order),
     )
 
 
@@ -91,7 +101,13 @@ def tile_recon_loss_pa_t_kernel(tc, X, A, B, C, out):
         c_turned = keep.tile([P, PASSES * N3 * PACK], BF16, align_bytes=64)
         b_flipped = turn_psum.tile([P, PASSES, HALVES, P], F32, tag="flipped")
         flip_words(nc, ident, b_raw, b_flipped[:])
-        copy_flipped(nc.vector.tensor_copy, b_flipped, b_turned, "row g u")
+        row_cols = PASSES * PACK
+        copy_flipped(
+            nc.vector.tensor_copy, b_flipped[:, :, :, 0:HEAD_ROWS], b_turned[:, 0 : HEAD_ROWS * row_cols], "row g u"
+        )
+        copy_flipped(
+            nc.scalar.copy, b_flipped[:, :, :, HEAD_ROWS:N2], b_turned[:, HEAD_ROWS * row_cols : N2 * row_cols], "row g u"
+        )
         a_bank = a_psum.tile([P, PASSES, N1, HALVES], F32)
         flip_words(nc, ident, a_raw, a_bank[:].rearrange("p g i u -> p g u i"))
         a_flipped = turn_psum.tile([P, PASSES, HALVES, P], F32, tag="flipped")
@@ -110,7 +126,14 @@ def tile_recon_loss_pa_t_kernel(tc, X, A, B, C, out):
             out=b_last[:],
             in_=b_turned[:].rearrange("p (n j g t) -> p n j g t", j=J_GROUP, g=PASSES, t=PACK)[:, :, J_GROUP - 1, :, :],
         )
-        copy_flipped(nc.scalar.copy, a_flipped, a_turned, "g row u")
+        copy_flipped(nc.scalar.copy, a_flipped[:], a_turned[:], "g row u")
+        b_extra = keep.tile([P, EXTRA_GROUPS, PASSES, PACK], F32)
+        nc.gpsimd.tensor_copy(
+            out=b_extra[:],
+            in_=b_turned[:].rearrange("p (n j g t) -> p n j g t", j=J_GROUP, g=PASSES, t=PACK)[
+                :, GROUPS - EXTRA_GROUPS : GROUPS, J_GROUP - 2, :, :
+            ],
+        )
 
         c_codes = keep.tile([P, PASSES * N3], U32, align_bytes=64)
         c_scales = keep.tile([P, PASSES * N3], U8, align_bytes=64)
@@ -125,7 +148,7 @@ def tile_recon_loss_pa_t_kernel(tc, X, A, B, C, out):
             )
 
         def multiply_on_vector(n):
-            j_count = J_GROUP - 1 if scalar_helps(n) else J_GROUP
+            j_count = J_GROUP - scalar_j(n) - gpsimd_j(n)
             j_rows = slice(n * J_GROUP, n * J_GROUP + j_count)
             shape = [P, j_count, PASSES, N1, PACK]
             nc.vector.tensor_tensor(
@@ -137,12 +160,21 @@ def tile_recon_loss_pa_t_kernel(tc, X, A, B, C, out):
                 op=mybir.AluOpType.mult,
             )
 
+        def multiply_on_gpsimd(n, j):
+            shape = [P, PASSES, N1, PACK]
+            nc.gpsimd.tensor_tensor(
+                out=product_of[n][:, j * J_COLS : (j + 1) * J_COLS].rearrange("p (g i t) -> p g i t", g=PASSES, t=PACK),
+                in0=a_view,
+                in1=b_view[:, n * J_GROUP + j, :, :].unsqueeze(2).to_broadcast(shape),
+                op=mybir.AluOpType.mult,
+            )
+
         planes_waiting = []
 
         def regroup_on_tensor():
             for entry in planes_waiting:
-                n, planes, regrouped = entry
-                if tensor_regroups(n) and regrouped is None:
+                n, j, planes, regrouped = entry
+                if tensor_regroups(n, j) and regrouped is None:
                     regrouped = turn_psum.tile([P, PASSES, N1 * PACK], BF16, tag="flipped")
                     for g in range(PASSES):
                         nc.tensor.matmul(
@@ -152,22 +184,21 @@ def tile_recon_loss_pa_t_kernel(tc, X, A, B, C, out):
                             start=True,
                             stop=True,
                         )
-                    entry[2] = regrouped
+                    entry[3] = regrouped
 
         def finish_on_scalar():
-            n, planes, regrouped = planes_waiting.pop(0)
-            last_j = product_of[n][:, (J_GROUP - 1) * J_COLS : GROUP_COLS]
-            if tensor_regroups(n):
-                nc.scalar.copy(out=last_j, in_=regrouped[:].rearrange("p g c -> p (g c)"))
+            n, j, planes, regrouped = planes_waiting.pop(0)
+            j_part = product_of[n][:, j * J_COLS : (j + 1) * J_COLS]
+            if tensor_regroups(n, j):
+                nc.scalar.copy(out=j_part, in_=regrouped[:].rearrange("p g c -> p (g c)"))
             else:
                 nc.scalar.copy(
-                    out=last_j.rearrange("p (g i t) -> p g i t", g=PASSES, t=PACK),
+                    out=j_part.rearrange("p (g i t) -> p g i t", g=PASSES, t=PACK),
                     in_=planes[:].rearrange("p g t i -> p g i t"),
                 )
 
-        def multiply_on_scalar(n, may_wait):
-            if not scalar_helps(n):
-                return
+        def multiply_on_scalar(n, j, may_wait):
+            b_of_j = b_last[:, n, :, :] if j == J_GROUP - 1 else b_extra[:, n - (GROUPS - EXTRA_GROUPS), :, :]
             planes = scalar_work.tile([P, PASSES, PACK, N1], BF16, bufs=PLANES_BUFS)
             for g in range(PASSES):
                 for t in range(PACK):
@@ -175,9 +206,9 @@ def tile_recon_loss_pa_t_kernel(tc, X, A, B, C, out):
                         out=planes[:, g, t, :],
                         in_=a_view[:, g, :, t],
                         func=mybir.ActivationFunctionType.Copy,
-                        scale=b_last[:, n, g, t : t + 1],
+                        scale=b_of_j[:, g, t : t + 1],
                     )
-            planes_waiting.append([n, planes, None])
+            planes_waiting.append([n, j, planes, None])
             if len(planes_waiting) > may_wait:
                 finish_on_scalar()
 
@@ -239,13 +270,11 @@ def tile_recon_loss_pa_t_kernel(tc, X, A, B, C, out):
             new_product(n)
         multiply_on_vector(0)
         multiply_on_vector(1)
-        multiply_on_scalar(1, 1)
-        copy_flipped(nc.scalar.copy, c_flipped, c_turned, "g row u")
-        regroup_on_tensor()
-        finish_on_scalar()
+        multiply_on_gpsimd(1, J_GROUP - 1)
+        copy_flipped(nc.scalar.copy, c_flipped[:], c_turned[:], "g row u")
         for n in range(2, 5):
-            multiply_on_scalar(n, 1)
-        multiply_on_scalar(5, 2)
+            multiply_on_scalar(n, J_GROUP - 1, 1)
+        multiply_on_scalar(5, J_GROUP - 1, 2)
         nc.vector.quantize_mx(out=c_codes[:].bitcast(FP8X4), scales=c_scales[:], in_=c_turned[:])
 
         emptied_before = None
@@ -268,7 +297,9 @@ def tile_recon_loss_pa_t_kernel(tc, X, A, B, C, out):
             for n in pair:
                 if n + 6 < GROUPS:
                     new_product(n + 6)
-                    multiply_on_scalar(n + 6, 2)
+                    multiply_on_scalar(n + 6, J_GROUP - 1, 2)
+                elif n + 4 < GROUPS and scalar_j(n + 4) == 2:
+                    multiply_on_scalar(n + 4, J_GROUP - 2, 2)
                 elif planes_waiting:
                     finish_on_scalar()
         for n, sums in kept_sums:

@@ -24,7 +24,7 @@ GROUP_COLS = J_GROUP * J_COLS
 GROUP_WORDS = GROUP_COLS // PACK
 GROUP_OUT = J_GROUP * N3
 STEPS = GROUPS // 2
-VECTOR_TAIL_STEPS = 2
+SHARED_I = 120
 SLOTS = 8
 SLOT_BYTES = GROUP_COLS * 2
 PLANES_BUFS = 5
@@ -48,22 +48,22 @@ def gpsimd_j(n):
     return 1 if n == 1 else 0
 
 
+def gpsimd_first_i(n):
+    return SHARED_I if n > SLOTS and n % 2 == 1 else N1
+
+
 def tensor_regroups(n, j):
     return n % 3 == 1 and j == J_GROUP - 1
 
 
 def flip_words(nc, ident, raw, flipped):
-    words = raw[:].bitcast(F32).rearrange("row (g p u) -> row g u p", g=PASSES, u=HALVES)
-    for g in range(PASSES):
-        for u in range(HALVES):
-            nc.tensor.transpose(flipped[:, g, u, :], words[:, g, u, :], ident[:])
+    words = raw[:].bitcast(F32).rearrange("row (p u) -> row u p", u=HALVES)
+    for u in range(HALVES):
+        nc.tensor.transpose(flipped[:, u, :], words[:, u, :], ident[:])
 
 
 def copy_flipped(copy, flipped, turned, order):
-    copy(
-        out=turned.bitcast(F32).rearrange("p (%s) -> p %s" % (order, order), g=PASSES, u=HALVES),
-        in_=flipped.rearrange("p g u row -> p %s" % order),
-    )
+    copy(out=turned.rearrange("p g row u -> p %s" % order), in_=flipped.rearrange("p g u row -> p %s" % order))
 
 
 def tile_recon_loss_pa_t_kernel(tc, X, A, B, C, out):
@@ -78,12 +78,12 @@ def tile_recon_loss_pa_t_kernel(tc, X, A, B, C, out):
     ) as turn_psum, tc.psum_pool(name="a_psum", bufs=1) as a_psum, tc.psum_pool(
         name="sums", bufs=5
     ) as sums_psum, tc.manual_schedule():
-        a_raw = keep.tile([P, R], BF16)
-        b_raw = keep.tile([P, R], BF16)
-        c_raw = keep.tile([P, R], BF16)
-        nc.sync.dma_start(out=b_raw[:], in_=B[:, :])
-        nc.sync.dma_start(out=a_raw[:], in_=A[:, :])
-        nc.sync.dma_start(out=c_raw[:], in_=C[:, :])
+        raw = {}
+        for factor in ("a", "b", "c"):
+            for g in range(PASSES):
+                raw[factor, g] = keep.tile([P, K_PASS], BF16, name="%s_raw%d" % (factor, g))
+        for factor, g, rows in (("b", 0, B), ("a", 0, A), ("b", 1, B), ("a", 1, A), ("c", 0, C), ("c", 1, C)):
+            nc.sync.dma_start(out=raw[factor, g][:], in_=rows[:, g * K_PASS : (g + 1) * K_PASS])
         x_chunks = []
         for c in range(X_CHUNKS):
             x_chunk = keep.tile([P, X_CHUNK_J * N3], BF16, name="x_chunk%d" % c)
@@ -99,41 +99,40 @@ def tile_recon_loss_pa_t_kernel(tc, X, A, B, C, out):
         a_turned = keep.tile([P, PASSES * N1 * PACK], BF16)
         b_turned = keep.tile([P, N2 * PASSES * PACK], BF16)
         c_turned = keep.tile([P, PASSES * N3 * PACK], BF16, align_bytes=64)
-        b_flipped = turn_psum.tile([P, PASSES, HALVES, P], F32, tag="flipped")
-        flip_words(nc, ident, b_raw, b_flipped[:])
-        row_cols = PASSES * PACK
-        copy_flipped(
-            nc.vector.tensor_copy, b_flipped[:, :, :, 0:HEAD_ROWS], b_turned[:, 0 : HEAD_ROWS * row_cols], "row g u"
-        )
-        copy_flipped(
-            nc.scalar.copy, b_flipped[:, :, :, HEAD_ROWS:N2], b_turned[:, HEAD_ROWS * row_cols : N2 * row_cols], "row g u"
-        )
-        a_bank = a_psum.tile([P, PASSES, N1, HALVES], F32)
-        flip_words(nc, ident, a_raw, a_bank[:].rearrange("p g i u -> p g u i"))
-        a_flipped = turn_psum.tile([P, PASSES, HALVES, P], F32, tag="flipped")
-        flip_words(nc, ident, a_raw, a_flipped[:])
-        c_flipped = turn_psum.tile([P, PASSES, HALVES, P], F32, tag="flipped")
-        flip_words(nc, ident, c_raw, c_flipped[:])
         a_view = a_turned[:].rearrange("p (g i t) -> p g i t", g=PASSES, t=PACK)
         b_view = b_turned[:].rearrange("p (j g t) -> p j g t", g=PASSES, t=PACK)
+        a_words = a_turned[:].bitcast(F32).rearrange("p (g row u) -> p g row u", g=PASSES, u=HALVES)
+        b_words = b_turned[:].bitcast(F32).rearrange("p (row g u) -> p g row u", g=PASSES, u=HALVES)
+        c_words = c_turned[:].bitcast(F32).rearrange("p (g row u) -> p g row u", g=PASSES, u=HALVES)
 
+        b_flipped = turn_psum.tile([P, PASSES, HALVES, P], F32, tag="flipped")
+        a_head = sums_psum.tile([P, N1, HALVES], F32, tag="sums")
+        a_bank = a_psum.tile([P, PASSES, N1, HALVES], F32)
+        a_flipped = sums_psum.tile([P, PASSES, HALVES, P], F32, tag="sums")
+        c_flipped = sums_psum.tile([P, PASSES, HALVES, P], F32, tag="sums")
+        def copy_b(copy, passes, rows):
+            copy_flipped(copy, b_flipped[:, passes, :, rows], b_words[:, passes, rows, :], "row g u")
+
+        flip_words(nc, ident, raw["b", 0], b_flipped[:, 0, :, :])
+        copy_b(nc.vector.tensor_copy, slice(0, 1), slice(0, HEAD_ROWS))
+        flip_words(nc, ident, raw["a", 0], a_head[:].rearrange("p i u -> p u i"))
+        flip_words(nc, ident, raw["b", 1], b_flipped[:, 1, :, :])
+        for g in range(PASSES):
+            flip_words(nc, ident, raw["a", g], a_bank[:, g, :, :].rearrange("p i u -> p u i"))
+        for g in range(PASSES):
+            flip_words(nc, ident, raw["a", g], a_flipped[:, g, :, :])
+        for g in range(PASSES):
+            flip_words(nc, ident, raw["c", g], c_flipped[:, g, :, :])
+        a_head_view = a_head[:].rearrange("p i u -> p (i u)").bitcast(BF16).rearrange("p (i t) -> p i t", t=PACK)
         a_bank_view = (
             a_bank[:].rearrange("p g i u -> p (g i u)").bitcast(BF16).rearrange("p (g i t) -> p g i t", g=PASSES, t=PACK)
         )
 
         b_last = keep.tile([P, GROUPS, PASSES, PACK], F32)
-        nc.scalar.copy(
-            out=b_last[:],
-            in_=b_turned[:].rearrange("p (n j g t) -> p n j g t", j=J_GROUP, g=PASSES, t=PACK)[:, :, J_GROUP - 1, :, :],
-        )
-        copy_flipped(nc.scalar.copy, a_flipped[:], a_turned[:], "g row u")
+        b_groups = b_turned[:].rearrange("p (n j g t) -> p n j g t", j=J_GROUP, g=PASSES, t=PACK)
+        copy_b(nc.scalar.copy, slice(1, 2), slice(0, HEAD_ROWS))
+        copy_b(nc.scalar.copy, slice(0, PASSES), slice(HEAD_ROWS, N2))
         b_extra = keep.tile([P, EXTRA_GROUPS, PASSES, PACK], F32)
-        nc.gpsimd.tensor_copy(
-            out=b_extra[:],
-            in_=b_turned[:].rearrange("p (n j g t) -> p n j g t", j=J_GROUP, g=PASSES, t=PACK)[
-                :, GROUPS - EXTRA_GROUPS : GROUPS, J_GROUP - 2, :, :
-            ],
-        )
 
         c_codes = keep.tile([P, PASSES * N3], U32, align_bytes=64)
         c_scales = keep.tile([P, PASSES * N3], U8, align_bytes=64)
@@ -148,17 +147,30 @@ def tile_recon_loss_pa_t_kernel(tc, X, A, B, C, out):
             )
 
         def multiply_on_vector(n):
+            multiply_i(nc.vector, a_bank_view, n, slice(0, gpsimd_first_i(n)))
+
+        def multiply_i(engine, a_source, n, i_range):
             j_count = J_GROUP - scalar_j(n) - gpsimd_j(n)
             j_rows = slice(n * J_GROUP, n * J_GROUP + j_count)
-            shape = [P, j_count, PASSES, N1, PACK]
-            nc.vector.tensor_tensor(
+            shape = [P, j_count, PASSES, i_range.stop - i_range.start, PACK]
+            engine.tensor_tensor(
                 out=product_of[n][:, 0 : j_count * J_COLS].rearrange(
                     "p (j g i t) -> p j g i t", j=j_count, g=PASSES, t=PACK
-                ),
-                in0=a_bank_view.unsqueeze(1).to_broadcast(shape),
+                )[:, :, :, i_range, :],
+                in0=a_source[:, :, i_range, :].unsqueeze(1).to_broadcast(shape),
                 in1=b_view[:, j_rows, :, :].unsqueeze(3).to_broadcast(shape),
                 op=mybir.AluOpType.mult,
             )
+
+        def multiply_pass_by_pass(n):
+            shape = [P, J_GROUP, N1, PACK]
+            for g in range(PASSES):
+                nc.vector.tensor_tensor(
+                    out=product_of[n][:].rearrange("p (j g i t) -> p g j i t", j=J_GROUP, g=PASSES, t=PACK)[:, g, :, :, :],
+                    in0=(a_head_view if g == 0 else a_bank_view[:, g, :, :]).unsqueeze(1).to_broadcast(shape),
+                    in1=b_view[:, n * J_GROUP : (n + 1) * J_GROUP, g, :].unsqueeze(2).to_broadcast(shape),
+                    op=mybir.AluOpType.mult,
+                )
 
         def multiply_on_gpsimd(n, j):
             shape = [P, PASSES, N1, PACK]
@@ -212,15 +224,21 @@ def tile_recon_loss_pa_t_kernel(tc, X, A, B, C, out):
             if len(planes_waiting) > may_wait:
                 finish_on_scalar()
 
-        def quantise(n):
+        def quantise(part):
+            n, first_j, j_count = part
             codes = work.tile([P, GROUP_WORDS], U32, align_bytes=64)
             scales = work.tile([P, GROUP_WORDS], U8, align_bytes=64)
-            nc.vector.quantize_mx(out=codes[:].bitcast(FP8X4), scales=scales[:], in_=product_of[n][:])
+            words = slice(0, j_count * J_COLS // PACK)
+            nc.vector.quantize_mx(
+                out=codes[:, words].bitcast(FP8X4),
+                scales=scales[:, words],
+                in_=product_of[n][:, first_j * J_COLS : (first_j + j_count) * J_COLS],
+            )
             return codes, scales
 
-        def contract(codes, scales):
-            sums = sums_psum.tile([P, J_GROUP, N3], F32)
-            for j in range(J_GROUP):
+        def contract(part, codes, scales):
+            sums = sums_psum.tile([P, J_GROUP, N3], F32, tag="sums")
+            for j in range(part[2]):
                 for g in range(PASSES):
                     i_cols = slice((j * PASSES + g) * N1, (j * PASSES + g + 1) * N1)
                     k_cols = slice(g * N3, (g + 1) * N3)
@@ -235,72 +253,80 @@ def tile_recon_loss_pa_t_kernel(tc, X, A, B, C, out):
                     )
             return sums
 
-        def x_part(first_group, groups):
-            first = (first_group * J_GROUP % X_CHUNK_J) * N3
-            return x_chunks[first_group * J_GROUP // X_CHUNK_J][:, first : first + groups * GROUP_OUT]
-
-        def subtract_on_vector(n, sums):
-            residual = work.tile([P, GROUP_OUT], F32)
-            nc.vector.tensor_tensor(
-                out=residual[:],
-                in0=sums[:].rearrange("p j k -> p (j k)"),
-                in1=x_part(n, 1),
-                op=mybir.AluOpType.subtract,
+        def subtract(engine, part, sums, residual):
+            n, first_j, j_count = part
+            first_j += n * J_GROUP
+            x_cols = slice(first_j % X_CHUNK_J * N3, (first_j % X_CHUNK_J + j_count) * N3)
+            engine.tensor_tensor(
+                out=residual, in0=sums, in1=x_chunks[first_j // X_CHUNK_J][:, x_cols], op=mybir.AluOpType.subtract
             )
-            nc.sync.dma_start(out=out_rows[:, n * GROUP_OUT : (n + 1) * GROUP_OUT], in_=residual[:])
+            nc.sync.dma_start(out=out_rows[:, first_j * N3 : (first_j + j_count) * N3], in_=residual)
 
-        def empty_on_scalar(pair_sums):
+        def subtract_on_vector(part, sums):
+            residual = work.tile([P, GROUP_OUT], F32)
+            cols = slice(0, part[2] * N3)
+            subtract(nc.vector, part, sums[:].rearrange("p j k -> p (j k)")[:, cols], residual[:, cols])
+
+        def empty_on_scalar(group_sums):
             emptied = scalar_work.tile([P, 2 * GROUP_OUT], F32)
-            for half in range(2):
+            for place, sums in enumerate(group_sums):
                 nc.scalar.copy(
-                    out=emptied[:, half * GROUP_OUT : (half + 1) * GROUP_OUT],
-                    in_=pair_sums[half][:].rearrange("p j k -> p (j k)"),
+                    out=emptied[:, place * GROUP_OUT : (place + 1) * GROUP_OUT],
+                    in_=sums[:].rearrange("p j k -> p (j k)"),
                 )
             return emptied
 
-        def subtract_on_gpsimd(step, emptied, slot):
+        def subtract_on_gpsimd(part, emptied):
             residual_pair = scalar_work.tile([P, 2 * GROUP_OUT], F32)
-            nc.gpsimd.tensor_tensor(
-                out=residual_pair[:], in0=emptied[:], in1=x_part(2 * step, 2), op=mybir.AluOpType.subtract
-            )
-            cols = slice(2 * step * GROUP_OUT, (2 * step + 2) * GROUP_OUT)
-            nc.sync.dma_start(out=out_rows[:, cols], in_=residual_pair[:])
+            cols = slice(0, part[2] * N3)
+            subtract(nc.gpsimd, part, emptied[:, cols], residual_pair[:, cols])
 
-        for n in range(6):
+        for n in range(SLOTS):
             new_product(n)
-        multiply_on_vector(0)
+        multiply_pass_by_pass(0)
+        nc.scalar.copy(out=b_last[:], in_=b_groups[:, :, J_GROUP - 1, :, :])
+        copy_flipped(nc.scalar.copy, a_flipped[:], a_words, "g row u")
         multiply_on_vector(1)
         multiply_on_gpsimd(1, J_GROUP - 1)
-        copy_flipped(nc.scalar.copy, c_flipped[:], c_turned[:], "g row u")
+        nc.gpsimd.tensor_copy(out=b_extra[:], in_=b_groups[:, GROUPS - EXTRA_GROUPS : GROUPS, J_GROUP - 2, :, :])
+        copy_flipped(nc.scalar.copy, c_flipped[:], c_words, "g row u")
         for n in range(2, 5):
             multiply_on_scalar(n, J_GROUP - 1, 1)
         multiply_on_scalar(5, J_GROUP - 1, 2)
         nc.vector.quantize_mx(out=c_codes[:].bitcast(FP8X4), scales=c_scales[:], in_=c_turned[:])
 
         emptied_before = None
-        kept_sums = []
         for step in range(STEPS):
             pair = (2 * step, 2 * step + 1)
-            quantised = [quantise(n) for n in pair]
-            pair_sums = [contract(codes, scales) for codes, scales in quantised]
+            parts = []
+            for n in pair:
+                parts.extend([(n, 0, 2), (n, 2, 2)] if n == GROUPS - 1 else [(n, 0, J_GROUP)])
+            quantised = [quantise(part) for part in parts]
+            part_sums = [contract(part, codes, scales) for part, (codes, scales) in zip(parts, quantised)]
             regroup_on_tensor()
+            for n in pair:
+                if n + SLOTS < GROUPS:
+                    new_product(n + SLOTS)
+                    if gpsimd_first_i(n + SLOTS) < N1:
+                        multiply_i(nc.gpsimd, a_view, n + SLOTS, slice(gpsimd_first_i(n + SLOTS), N1))
             if emptied_before is not None:
-                subtract_on_gpsimd(step - 1, emptied_before, pair[1] % SLOTS)
+                subtract_on_gpsimd((2 * step - 2, 0, 2 * J_GROUP), emptied_before)
                 emptied_before = None
             for n in pair:
                 if n + 2 < GROUPS:
                     multiply_on_vector(n + 2)
-            if step < STEPS - VECTOR_TAIL_STEPS:
-                emptied_before = empty_on_scalar(pair_sums)
+            if step < STEPS - 2:
+                emptied_before = empty_on_scalar(part_sums)
+            elif step == STEPS - 2:
+                subtract_on_gpsimd(parts[0], empty_on_scalar(part_sums[0:1]))
+                subtract_on_vector(parts[1], part_sums[1])
             else:
-                kept_sums.extend(zip(pair, pair_sums))
+                for part, sums in zip(parts, part_sums):
+                    subtract_on_vector(part, sums)
             for n in pair:
                 if n + 6 < GROUPS:
-                    new_product(n + 6)
                     multiply_on_scalar(n + 6, J_GROUP - 1, 2)
                 elif n + 4 < GROUPS and scalar_j(n + 4) == 2:
                     multiply_on_scalar(n + 4, J_GROUP - 2, 2)
                 elif planes_waiting:
                     finish_on_scalar()
-        for n, sums in kept_sums:
-            subtract_on_vector(n, sums)

@@ -25,6 +25,7 @@ GROUP_WORDS = GROUP_COLS // PACK
 GROUP_OUT = J_GROUP * N3
 STEPS = GROUPS // 2
 SHARED_I = 120
+RUN = 4
 SLOTS = 8
 SLOT_BYTES = GROUP_COLS * 2
 PLANES_BUFS = 5
@@ -96,6 +97,7 @@ def tile_recon_loss_pa_t_kernel(tc, X, A, B, C, out):
         ident_bf = keep.tile([P, P], BF16)
         make_identity(nc, ident_bf[:])
 
+        a_planes = keep.tile([P, PASSES, PACK, N1], BF16)
         a_turned = keep.tile([P, PASSES * N1 * PACK], BF16)
         b_turned = keep.tile([P, N2 * PASSES * PACK], BF16)
         c_turned = keep.tile([P, PASSES * N3 * PACK], BF16, align_bytes=64)
@@ -123,6 +125,11 @@ def tile_recon_loss_pa_t_kernel(tc, X, A, B, C, out):
             flip_words(nc, ident, raw["a", g], a_flipped[:, g, :, :])
         for g in range(PASSES):
             flip_words(nc, ident, raw["c", g], c_flipped[:, g, :, :])
+        planes_flipped = sums_psum.tile([P, PASSES, PACK, N1], BF16, tag="sums")
+        for g in range(PASSES):
+            columns = raw["a", g][:].rearrange("i (p t) -> i t p", t=PACK)
+            for t in range(PACK):
+                nc.tensor.transpose(planes_flipped[:, g, t, :], columns[:, t, :], ident_bf[:])
         a_head_view = a_head[:].rearrange("p i u -> p (i u)").bitcast(BF16).rearrange("p (i t) -> p i t", t=PACK)
         a_bank_view = (
             a_bank[:].rearrange("p g i u -> p (g i u)").bitcast(BF16).rearrange("p (g i t) -> p g i t", g=PASSES, t=PACK)
@@ -192,7 +199,7 @@ def tile_recon_loss_pa_t_kernel(tc, X, A, B, C, out):
                         nc.tensor.matmul(
                             out=regrouped[:, g, :],
                             lhsT=ident_bf[:],
-                            rhs=planes[:, g, :, :].rearrange("p t i -> p i t"),
+                            rhs=planes[:, :, g, :].rearrange("p t i -> p i t"),
                             start=True,
                             stop=True,
                         )
@@ -205,18 +212,18 @@ def tile_recon_loss_pa_t_kernel(tc, X, A, B, C, out):
                 nc.scalar.copy(out=j_part, in_=regrouped[:].rearrange("p g c -> p (g c)"))
             else:
                 nc.scalar.copy(
-                    out=j_part.rearrange("p (g i t) -> p g i t", g=PASSES, t=PACK),
-                    in_=planes[:].rearrange("p g t i -> p g i t"),
+                    out=j_part.rearrange("p (c i t) -> p c t i", i=RUN, t=PACK),
+                    in_=planes[:].rearrange("p t g i -> p t (g i)").rearrange("p t (c i) -> p c t i", i=RUN),
                 )
 
         def multiply_on_scalar(n, j, may_wait):
             b_of_j = b_last[:, n, :, :] if j == J_GROUP - 1 else b_extra[:, n - (GROUPS - EXTRA_GROUPS), :, :]
-            planes = scalar_work.tile([P, PASSES, PACK, N1], BF16, bufs=PLANES_BUFS)
+            planes = scalar_work.tile([P, PACK, PASSES, N1], BF16, bufs=PLANES_BUFS)
             for g in range(PASSES):
                 for t in range(PACK):
                     nc.scalar.activation(
-                        out=planes[:, g, t, :],
-                        in_=a_view[:, g, :, t],
+                        out=planes[:, t, g, :],
+                        in_=a_planes[:, g, t, :],
                         func=mybir.ActivationFunctionType.Copy,
                         scale=b_of_j[:, g, t : t + 1],
                     )
@@ -290,6 +297,7 @@ def tile_recon_loss_pa_t_kernel(tc, X, A, B, C, out):
         multiply_on_gpsimd(1, J_GROUP - 1)
         nc.gpsimd.tensor_copy(out=b_extra[:], in_=b_groups[:, GROUPS - EXTRA_GROUPS : GROUPS, J_GROUP - 2, :, :])
         copy_flipped(nc.scalar.copy, c_flipped[:], c_words, "g row u")
+        nc.scalar.copy(out=a_planes[:], in_=planes_flipped[:])
         for n in range(2, 5):
             multiply_on_scalar(n, J_GROUP - 1, 1)
         multiply_on_scalar(5, J_GROUP - 1, 2)

@@ -40,17 +40,17 @@ EXTRA_GROUPS = 2
 
 
 def scalar_j(n):
-    if n < 2:
+    if n == 0 or gpsimd_j(n):
         return 0
     return 2 if n >= GROUPS - EXTRA_GROUPS else 1
 
 
 def gpsimd_j(n):
-    return 1 if n == 1 else 0
+    return 1 if n in (1, SLOTS + 1) else 0
 
 
 def gpsimd_first_i(n):
-    return SHARED_I if n > SLOTS and n % 2 == 1 else N1
+    return SHARED_I if n > SLOTS + 1 and n % 2 == 1 else N1
 
 
 def tensor_regroups(n, j):
@@ -110,7 +110,7 @@ def tile_recon_loss_pa_t_kernel(tc, X, A, B, C, out):
         b_flipped = turn_psum.tile([P, PASSES, HALVES, P], F32, tag="flipped")
         a_head = sums_psum.tile([P, N1, HALVES], F32, tag="sums")
         a_bank = a_psum.tile([P, PASSES, N1, HALVES], F32)
-        a_flipped = sums_psum.tile([P, PASSES, HALVES, P], F32, tag="sums")
+        a_flipped = sums_psum.tile([P, HALVES, P], F32, tag="sums")
         c_flipped = sums_psum.tile([P, PASSES, HALVES, P], F32, tag="sums")
         def copy_b(copy, passes, rows):
             copy_flipped(copy, b_flipped[:, passes, :, rows], b_words[:, passes, rows, :], "row g u")
@@ -121,8 +121,7 @@ def tile_recon_loss_pa_t_kernel(tc, X, A, B, C, out):
         flip_words(nc, ident, raw["b", 1], b_flipped[:, 1, :, :])
         for g in range(PASSES):
             flip_words(nc, ident, raw["a", g], a_bank[:, g, :, :].rearrange("p i u -> p u i"))
-        for g in range(PASSES):
-            flip_words(nc, ident, raw["a", g], a_flipped[:, g, :, :])
+        flip_words(nc, ident, raw["a", 1], a_flipped[:])
         for g in range(PASSES):
             flip_words(nc, ident, raw["c", g], c_flipped[:, g, :, :])
         planes_flipped = sums_psum.tile([P, PASSES, PACK, N1], BF16, tag="sums")
@@ -180,13 +179,14 @@ def tile_recon_loss_pa_t_kernel(tc, X, A, B, C, out):
                 )
 
         def multiply_on_gpsimd(n, j):
-            shape = [P, PASSES, N1, PACK]
-            nc.gpsimd.tensor_tensor(
-                out=product_of[n][:, j * J_COLS : (j + 1) * J_COLS].rearrange("p (g i t) -> p g i t", g=PASSES, t=PACK),
-                in0=a_view,
-                in1=b_view[:, n * J_GROUP + j, :, :].unsqueeze(2).to_broadcast(shape),
-                op=mybir.AluOpType.mult,
-            )
+            of_j = product_of[n][:, j * J_COLS : (j + 1) * J_COLS].rearrange("p (g i t) -> p g i t", g=PASSES, t=PACK)
+            for g in range(PASSES):
+                nc.gpsimd.tensor_tensor(
+                    out=of_j[:, g, :, :],
+                    in0=a_view[:, g, :, :],
+                    in1=b_view[:, n * J_GROUP + j, g, :].unsqueeze(1).to_broadcast([P, N1, PACK]),
+                    op=mybir.AluOpType.mult,
+                )
 
         planes_waiting = []
 
@@ -283,16 +283,24 @@ def tile_recon_loss_pa_t_kernel(tc, X, A, B, C, out):
                 )
             return emptied
 
-        def subtract_on_gpsimd(part, emptied):
-            residual_pair = scalar_work.tile([P, 2 * GROUP_OUT], F32)
+        def subtract_on_gpsimd(part, emptied, freed_by=None):
+            if freed_by is None:
+                residual_pair = scalar_work.tile([P, 2 * GROUP_OUT], F32)
+            else:
+                slot = freed_by % SLOTS
+                residual_pair = products.tile(
+                    [P, 2 * GROUP_OUT], F32, name="residual%d" % slot, tag="residual%d" % slot,
+                    offset=slot * SLOT_BYTES, align_bytes=64,
+                )
             cols = slice(0, part[2] * N3)
             subtract(nc.gpsimd, part, emptied[:, cols], residual_pair[:, cols])
 
         for n in range(SLOTS):
             new_product(n)
         multiply_pass_by_pass(0)
+        nc.scalar.copy(out=a_words[:, 0, :, :], in_=a_head[:])
         nc.scalar.copy(out=b_last[:], in_=b_groups[:, :, J_GROUP - 1, :, :])
-        copy_flipped(nc.scalar.copy, a_flipped[:], a_words, "g row u")
+        nc.scalar.copy(out=a_words[:, 1, :, :], in_=a_flipped[:].rearrange("p u row -> p row u"))
         multiply_on_vector(1)
         multiply_on_gpsimd(1, J_GROUP - 1)
         nc.gpsimd.tensor_copy(out=b_extra[:], in_=b_groups[:, GROUPS - EXTRA_GROUPS : GROUPS, J_GROUP - 2, :, :])
@@ -315,10 +323,13 @@ def tile_recon_loss_pa_t_kernel(tc, X, A, B, C, out):
             for n in pair:
                 if n + SLOTS < GROUPS:
                     new_product(n + SLOTS)
+                    if gpsimd_j(n + SLOTS):
+                        multiply_on_gpsimd(n + SLOTS, J_GROUP - 1)
                     if gpsimd_first_i(n + SLOTS) < N1:
                         multiply_i(nc.gpsimd, a_view, n + SLOTS, slice(gpsimd_first_i(n + SLOTS), N1))
             if emptied_before is not None:
-                subtract_on_gpsimd((2 * step - 2, 0, 2 * J_GROUP), emptied_before)
+                freed_by = pair[1] if pair[1] + SLOTS >= GROUPS else None
+                subtract_on_gpsimd((2 * step - 2, 0, 2 * J_GROUP), emptied_before, freed_by)
                 emptied_before = None
             for n in pair:
                 if n + 2 < GROUPS:
@@ -333,7 +344,8 @@ def tile_recon_loss_pa_t_kernel(tc, X, A, B, C, out):
                     subtract_on_vector(part, sums)
             for n in pair:
                 if n + 6 < GROUPS:
-                    multiply_on_scalar(n + 6, J_GROUP - 1, 2)
+                    if scalar_j(n + 6):
+                        multiply_on_scalar(n + 6, J_GROUP - 1, 2)
                 elif n + 4 < GROUPS and scalar_j(n + 4) == 2:
                     multiply_on_scalar(n + 4, J_GROUP - 2, 2)
                 elif planes_waiting:

@@ -54,7 +54,7 @@ def gpsimd_first_i(n):
 
 
 def tensor_regroups(n, j):
-    return n % 3 == 1 and j == J_GROUP - 1
+    return n % 7 in (1, 4, 6) and j == J_GROUP - 1
 
 
 def flip_words(nc, ident, raw, flipped):
@@ -190,8 +190,8 @@ def tile_recon_loss_pa_t_kernel(tc, X, A, B, C, out):
 
         planes_waiting = []
 
-        def regroup_on_tensor():
-            for entry in planes_waiting:
+        def regroup_on_tensor(entries):
+            for entry in entries:
                 n, j, planes, regrouped = entry
                 if tensor_regroups(n, j) and regrouped is None:
                     regrouped = turn_psum.tile([P, PASSES, N1 * PACK], BF16, tag="flipped")
@@ -311,6 +311,16 @@ def tile_recon_loss_pa_t_kernel(tc, X, A, B, C, out):
         multiply_on_scalar(5, J_GROUP - 1, 2)
         nc.vector.quantize_mx(out=c_codes[:].bitcast(FP8X4), scales=c_scales[:], in_=c_turned[:])
 
+        def scalar_turn(n):
+            if n + 6 < GROUPS:
+                if scalar_j(n + 6):
+                    multiply_on_scalar(n + 6, J_GROUP - 1, 2)
+            elif n + 4 < GROUPS and scalar_j(n + 4) == 2:
+                multiply_on_scalar(n + 4, J_GROUP - 2, 2)
+            elif planes_waiting:
+                finish_on_scalar()
+
+        regroup_on_tensor(planes_waiting)
         emptied_before = None
         for step in range(STEPS):
             pair = (2 * step, 2 * step + 1)
@@ -319,7 +329,7 @@ def tile_recon_loss_pa_t_kernel(tc, X, A, B, C, out):
                 parts.extend([(n, 0, 2), (n, 2, 2)] if n == GROUPS - 1 else [(n, 0, J_GROUP)])
             quantised = [quantise(part) for part in parts]
             part_sums = [contract(part, codes, scales) for part, (codes, scales) in zip(parts, quantised)]
-            regroup_on_tensor()
+            regroup_on_tensor(planes_waiting)
             for n in pair:
                 if n + SLOTS < GROUPS:
                     new_product(n + SLOTS)
@@ -334,6 +344,7 @@ def tile_recon_loss_pa_t_kernel(tc, X, A, B, C, out):
             for n in pair:
                 if n + 2 < GROUPS:
                     multiply_on_vector(n + 2)
+            scalar_turn(pair[0])
             if step < STEPS - 2:
                 emptied_before = empty_on_scalar(part_sums)
             elif step == STEPS - 2:
@@ -342,11 +353,5 @@ def tile_recon_loss_pa_t_kernel(tc, X, A, B, C, out):
             else:
                 for part, sums in zip(parts, part_sums):
                     subtract_on_vector(part, sums)
-            for n in pair:
-                if n + 6 < GROUPS:
-                    if scalar_j(n + 6):
-                        multiply_on_scalar(n + 6, J_GROUP - 1, 2)
-                elif n + 4 < GROUPS and scalar_j(n + 4) == 2:
-                    multiply_on_scalar(n + 4, J_GROUP - 2, 2)
-                elif planes_waiting:
-                    finish_on_scalar()
+            scalar_turn(pair[1])
+            regroup_on_tensor(planes_waiting[:-1])

@@ -50,7 +50,7 @@ def gpsimd_j(n):
 
 
 def gpsimd_first_i(n):
-    return SHARED_I if n > SLOTS + 1 and n % 2 == 1 else N1
+    return SHARED_I if n > SLOTS + 1 and n % 2 == 0 else N1
 
 
 def tensor_regroups(n, j):

import concourse.mybir as mybir
from concourse.masks import make_identity

BF16 = mybir.dt.bfloat16
F32 = mybir.dt.float32
U32 = mybir.dt.uint32
U8 = mybir.dt.uint8
FP8X4 = mybir.dt.float8_e4m3fn_x4

P = 128
PACK = 4
K_PASS = P * PACK
N1 = 128
N2 = 128
N3 = 128
R = 1024
PASSES = R // K_PASS
HALVES = PACK // 2

J_GROUP = 4
GROUPS = N2 // J_GROUP
J_COLS = PASSES * N1 * PACK
GROUP_COLS = J_GROUP * J_COLS
GROUP_WORDS = GROUP_COLS // PACK
GROUP_OUT = J_GROUP * N3
STEPS = GROUPS // 2
SHARED_I = 120
RUN = 4
SLOTS = 8
SLOT_BYTES = GROUP_COLS * 2
PLANES_BUFS = 5
X_CHUNK_J = 16
X_CHUNKS = N2 // X_CHUNK_J

FLOPS = 2 * N1 * N2 * N3 * R


HEAD_ROWS = 12
EXTRA_GROUPS = 2


def scalar_j(n):
    if n == 0 or gpsimd_j(n):
        return 0
    return 2 if n >= GROUPS - EXTRA_GROUPS else 1


def gpsimd_j(n):
    return 1 if n in (1, SLOTS + 1) else 0


def gpsimd_first_i(n):
    return SHARED_I if n > SLOTS + 1 and n % 2 == 0 else N1


def tensor_regroups(n, j):
    return n % 7 in (1, 4, 6) and j == J_GROUP - 1


def flip_words(nc, ident, raw, flipped):
    words = raw[:].bitcast(F32).rearrange("row (p u) -> row u p", u=HALVES)
    for u in range(HALVES):
        nc.tensor.transpose(flipped[:, u, :], words[:, u, :], ident[:])


def copy_flipped(copy, flipped, turned, order):
    copy(out=turned.rearrange("p g row u -> p %s" % order), in_=flipped.rearrange("p g u row -> p %s" % order))


def tile_recon_loss_pa_t_kernel(tc, X, A, B, C, out):
    nc = tc.nc
    x_rows = X.rearrange("i j k -> i (j k)")
    out_rows = out.rearrange("i j k -> i (j k)")

    with tc.tile_pool(name="keep", bufs=1) as keep, tc.tile_pool(name="work", bufs=4) as work, tc.tile_pool(
        name="products", bufs=1
    ) as products, tc.tile_pool(name="scalar_work", bufs=3) as scalar_work, tc.psum_pool(
        name="turn", bufs=2
    ) as turn_psum, tc.psum_pool(name="a_psum", bufs=1) as a_psum, tc.psum_pool(
        name="sums", bufs=5
    ) as sums_psum, tc.manual_schedule():
        raw = {}
        for factor in ("a", "b", "c"):
            for g in range(PASSES):
                raw[factor, g] = keep.tile([P, K_PASS], BF16, name="%s_raw%d" % (factor, g))
        for factor, g, rows in (("b", 0, B), ("a", 0, A), ("b", 1, B), ("a", 1, A), ("c", 0, C), ("c", 1, C)):
            nc.sync.dma_start(out=raw[factor, g][:], in_=rows[:, g * K_PASS : (g + 1) * K_PASS])
        x_chunks = []
        for c in range(X_CHUNKS):
            x_chunk = keep.tile([P, X_CHUNK_J * N3], BF16, name="x_chunk%d" % c)
            cols = slice(c * X_CHUNK_J * N3, (c + 1) * X_CHUNK_J * N3)
            nc.sync.dma_start(out=x_chunk[:], in_=x_rows[:, cols])
            x_chunks.append(x_chunk)

        ident = keep.tile([P, P], F32)
        make_identity(nc, ident[:])
        ident_bf = keep.tile([P, P], BF16)
        make_identity(nc, ident_bf[:])

        a_planes = keep.tile([P, PASSES, PACK, N1], BF16)
        a_turned = keep.tile([P, PASSES * N1 * PACK], BF16)
        b_turned = keep.tile([P, N2 * PASSES * PACK], BF16)
        c_turned = keep.tile([P, PASSES * N3 * PACK], BF16, align_bytes=64)
        a_view = a_turned[:].rearrange("p (g i t) -> p g i t", g=PASSES, t=PACK)
        b_view = b_turned[:].rearrange("p (j g t) -> p j g t", g=PASSES, t=PACK)
        a_words = a_turned[:].bitcast(F32).rearrange("p (g row u) -> p g row u", g=PASSES, u=HALVES)
        b_words = b_turned[:].bitcast(F32).rearrange("p (row g u) -> p g row u", g=PASSES, u=HALVES)
        c_words = c_turned[:].bitcast(F32).rearrange("p (g row u) -> p g row u", g=PASSES, u=HALVES)

        b_flipped = turn_psum.tile([P, PASSES, HALVES, P], F32, tag="flipped")
        a_head = sums_psum.tile([P, N1, HALVES], F32, tag="sums")
        a_bank = a_psum.tile([P, PASSES, N1, HALVES], F32)
        a_flipped = sums_psum.tile([P, HALVES, P], F32, tag="sums")
        c_flipped = sums_psum.tile([P, PASSES, HALVES, P], F32, tag="sums")
        def copy_b(copy, passes, rows):
            copy_flipped(copy, b_flipped[:, passes, :, rows], b_words[:, passes, rows, :], "row g u")

        flip_words(nc, ident, raw["b", 0], b_flipped[:, 0, :, :])
        copy_b(nc.vector.tensor_copy, slice(0, 1), slice(0, HEAD_ROWS))
        flip_words(nc, ident, raw["a", 0], a_head[:].rearrange("p i u -> p u i"))
        flip_words(nc, ident, raw["b", 1], b_flipped[:, 1, :, :])
        for g in range(PASSES):
            flip_words(nc, ident, raw["a", g], a_bank[:, g, :, :].rearrange("p i u -> p u i"))
        flip_words(nc, ident, raw["a", 1], a_flipped[:])
        for g in range(PASSES):
            flip_words(nc, ident, raw["c", g], c_flipped[:, g, :, :])
        planes_flipped = sums_psum.tile([P, PASSES, PACK, N1], BF16, tag="sums")
        for g in range(PASSES):
            columns = raw["a", g][:].rearrange("i (p t) -> i t p", t=PACK)
            for t in range(PACK):
                nc.tensor.transpose(planes_flipped[:, g, t, :], columns[:, t, :], ident_bf[:])
        a_head_view = a_head[:].rearrange("p i u -> p (i u)").bitcast(BF16).rearrange("p (i t) -> p i t", t=PACK)
        a_bank_view = (
            a_bank[:].rearrange("p g i u -> p (g i u)").bitcast(BF16).rearrange("p (g i t) -> p g i t", g=PASSES, t=PACK)
        )

        b_last = keep.tile([P, GROUPS, PASSES, PACK], F32)
        b_groups = b_turned[:].rearrange("p (n j g t) -> p n j g t", j=J_GROUP, g=PASSES, t=PACK)
        copy_b(nc.scalar.copy, slice(1, 2), slice(0, HEAD_ROWS))
        copy_b(nc.scalar.copy, slice(0, PASSES), slice(HEAD_ROWS, N2))
        b_extra = keep.tile([P, EXTRA_GROUPS, PASSES, PACK], F32)

        c_codes = keep.tile([P, PASSES * N3], U32, align_bytes=64)
        c_scales = keep.tile([P, PASSES * N3], U8, align_bytes=64)

        product_of = {}

        def new_product(n):
            slot = n % SLOTS
            product_of[n] = products.tile(
                [P, GROUP_COLS], BF16, name="product%d" % slot, tag="product%d" % slot,
                offset=slot * SLOT_BYTES, align_bytes=64,
            )

        def multiply_on_vector(n):
            multiply_i(nc.vector, a_bank_view, n, slice(0, gpsimd_first_i(n)))

        def multiply_i(engine, a_source, n, i_range):
            j_count = J_GROUP - scalar_j(n) - gpsimd_j(n)
            j_rows = slice(n * J_GROUP, n * J_GROUP + j_count)
            shape = [P, j_count, PASSES, i_range.stop - i_range.start, PACK]
            engine.tensor_tensor(
                out=product_of[n][:, 0 : j_count * J_COLS].rearrange(
                    "p (j g i t) -> p j g i t", j=j_count, g=PASSES, t=PACK
                )[:, :, :, i_range, :],
                in0=a_source[:, :, i_range, :].unsqueeze(1).to_broadcast(shape),
                in1=b_view[:, j_rows, :, :].unsqueeze(3).to_broadcast(shape),
                op=mybir.AluOpType.mult,
            )

        def multiply_pass_by_pass(n):
            shape = [P, J_GROUP, N1, PACK]
            for g in range(PASSES):
                nc.vector.tensor_tensor(
                    out=product_of[n][:].rearrange("p (j g i t) -> p g j i t", j=J_GROUP, g=PASSES, t=PACK)[:, g, :, :, :],
                    in0=(a_head_view if g == 0 else a_bank_view[:, g, :, :]).unsqueeze(1).to_broadcast(shape),
                    in1=b_view[:, n * J_GROUP : (n + 1) * J_GROUP, g, :].unsqueeze(2).to_broadcast(shape),
                    op=mybir.AluOpType.mult,
                )

        def multiply_on_gpsimd(n, j):
            of_j = product_of[n][:, j * J_COLS : (j + 1) * J_COLS].rearrange("p (g i t) -> p g i t", g=PASSES, t=PACK)
            for g in range(PASSES):
                nc.gpsimd.tensor_tensor(
                    out=of_j[:, g, :, :],
                    in0=a_view[:, g, :, :],
                    in1=b_view[:, n * J_GROUP + j, g, :].unsqueeze(1).to_broadcast([P, N1, PACK]),
                    op=mybir.AluOpType.mult,
                )

        planes_waiting = []

        def regroup_on_tensor(entries):
            for entry in entries:
                n, j, planes, regrouped = entry
                if tensor_regroups(n, j) and regrouped is None:
                    regrouped = turn_psum.tile([P, PASSES, N1 * PACK], BF16, tag="flipped")
                    for g in range(PASSES):
                        nc.tensor.matmul(
                            out=regrouped[:, g, :],
                            lhsT=ident_bf[:],
                            rhs=planes[:, :, g, :].rearrange("p t i -> p i t"),
                            start=True,
                            stop=True,
                        )
                    entry[3] = regrouped

        def finish_on_scalar():
            n, j, planes, regrouped = planes_waiting.pop(0)
            j_part = product_of[n][:, j * J_COLS : (j + 1) * J_COLS]
            if tensor_regroups(n, j):
                nc.scalar.copy(out=j_part, in_=regrouped[:].rearrange("p g c -> p (g c)"))
            else:
                nc.scalar.copy(
                    out=j_part.rearrange("p (c i t) -> p c t i", i=RUN, t=PACK),
                    in_=planes[:].rearrange("p t g i -> p t (g i)").rearrange("p t (c i) -> p c t i", i=RUN),
                )

        def multiply_on_scalar(n, j, may_wait):
            b_of_j = b_last[:, n, :, :] if j == J_GROUP - 1 else b_extra[:, n - (GROUPS - EXTRA_GROUPS), :, :]
            planes = scalar_work.tile([P, PACK, PASSES, N1], BF16, bufs=PLANES_BUFS)
            for g in range(PASSES):
                for t in range(PACK):
                    nc.scalar.activation(
                        out=planes[:, t, g, :],
                        in_=a_planes[:, g, t, :],
                        func=mybir.ActivationFunctionType.Copy,
                        scale=b_of_j[:, g, t : t + 1],
                    )
            planes_waiting.append([n, j, planes, None])
            if len(planes_waiting) > may_wait:
                finish_on_scalar()

        def quantise(part):
            n, first_j, j_count = part
            codes = work.tile([P, GROUP_WORDS], U32, align_bytes=64)
            scales = work.tile([P, GROUP_WORDS], U8, align_bytes=64)
            words = slice(0, j_count * J_COLS // PACK)
            nc.vector.quantize_mx(
                out=codes[:, words].bitcast(FP8X4),
                scales=scales[:, words],
                in_=product_of[n][:, first_j * J_COLS : (first_j + j_count) * J_COLS],
            )
            return codes, scales

        def contract(part, codes, scales):
            sums = sums_psum.tile([P, J_GROUP, N3], F32, tag="sums")
            for j in range(part[2]):
                for g in range(PASSES):
                    i_cols = slice((j * PASSES + g) * N1, (j * PASSES + g + 1) * N1)
                    k_cols = slice(g * N3, (g + 1) * N3)
                    nc.tensor.matmul_mx(
                        out=sums[:, j, :],
                        lhsT=codes[:, i_cols].bitcast(FP8X4),
                        lhsT_scale=scales[:, i_cols],
                        rhs=c_codes[:, k_cols].bitcast(FP8X4),
                        rhs_scale=c_scales[:, k_cols],
                        start=(g == 0),
                        stop=(g == PASSES - 1),
                    )
            return sums

        def subtract(engine, part, sums, residual):
            n, first_j, j_count = part
            first_j += n * J_GROUP
            x_cols = slice(first_j % X_CHUNK_J * N3, (first_j % X_CHUNK_J + j_count) * N3)
            engine.tensor_tensor(
                out=residual, in0=sums, in1=x_chunks[first_j // X_CHUNK_J][:, x_cols], op=mybir.AluOpType.subtract
            )
            nc.sync.dma_start(out=out_rows[:, first_j * N3 : (first_j + j_count) * N3], in_=residual)

        def subtract_on_vector(part, sums):
            residual = work.tile([P, GROUP_OUT], F32)
            cols = slice(0, part[2] * N3)
            subtract(nc.vector, part, sums[:].rearrange("p j k -> p (j k)")[:, cols], residual[:, cols])

        def empty_on_scalar(group_sums):
            emptied = scalar_work.tile([P, 2 * GROUP_OUT], F32)
            for place, sums in enumerate(group_sums):
                nc.scalar.copy(
                    out=emptied[:, place * GROUP_OUT : (place + 1) * GROUP_OUT],
                    in_=sums[:].rearrange("p j k -> p (j k)"),
                )
            return emptied

        def subtract_on_gpsimd(part, emptied, freed_by=None):
            if freed_by is None:
                residual_pair = scalar_work.tile([P, 2 * GROUP_OUT], F32)
            else:
                slot = freed_by % SLOTS
                residual_pair = products.tile(
                    [P, 2 * GROUP_OUT], F32, name="residual%d" % slot, tag="residual%d" % slot,
                    offset=slot * SLOT_BYTES, align_bytes=64,
                )
            cols = slice(0, part[2] * N3)
            subtract(nc.gpsimd, part, emptied[:, cols], residual_pair[:, cols])

        for n in range(SLOTS):
            new_product(n)
        multiply_pass_by_pass(0)
        nc.scalar.copy(out=a_words[:, 0, :, :], in_=a_head[:])
        nc.scalar.copy(out=b_last[:], in_=b_groups[:, :, J_GROUP - 1, :, :])
        nc.scalar.copy(out=a_words[:, 1, :, :], in_=a_flipped[:].rearrange("p u row -> p row u"))
        multiply_on_vector(1)
        multiply_on_gpsimd(1, J_GROUP - 1)
        nc.gpsimd.tensor_copy(out=b_extra[:], in_=b_groups[:, GROUPS - EXTRA_GROUPS : GROUPS, J_GROUP - 2, :, :])
        copy_flipped(nc.scalar.copy, c_flipped[:], c_words, "g row u")
        nc.scalar.copy(out=a_planes[:], in_=planes_flipped[:])
        for n in range(2, 5):
            multiply_on_scalar(n, J_GROUP - 1, 1)
        multiply_on_scalar(5, J_GROUP - 1, 2)
        nc.vector.quantize_mx(out=c_codes[:].bitcast(FP8X4), scales=c_scales[:], in_=c_turned[:])

        def scalar_turn(n):
            if n + 6 < GROUPS:
                if scalar_j(n + 6):
                    multiply_on_scalar(n + 6, J_GROUP - 1, 2)
            elif n + 4 < GROUPS and scalar_j(n + 4) == 2:
                multiply_on_scalar(n + 4, J_GROUP - 2, 2)
            elif planes_waiting:
                finish_on_scalar()

        regroup_on_tensor(planes_waiting)
        emptied_before = None
        for step in range(STEPS):
            pair = (2 * step, 2 * step + 1)
            parts = []
            for n in pair:
                parts.extend([(n, 0, 2), (n, 2, 2)] if n == GROUPS - 1 else [(n, 0, J_GROUP)])
            quantised = [quantise(part) for part in parts]
            part_sums = [contract(part, codes, scales) for part, (codes, scales) in zip(parts, quantised)]
            regroup_on_tensor(planes_waiting)
            for n in pair:
                if n + SLOTS < GROUPS:
                    new_product(n + SLOTS)
                    if gpsimd_j(n + SLOTS):
                        multiply_on_gpsimd(n + SLOTS, J_GROUP - 1)
                    if gpsimd_first_i(n + SLOTS) < N1:
                        multiply_i(nc.gpsimd, a_view, n + SLOTS, slice(gpsimd_first_i(n + SLOTS), N1))
            if emptied_before is not None:
                freed_by = pair[1] if pair[1] + SLOTS >= GROUPS else None
                subtract_on_gpsimd((2 * step - 2, 0, 2 * J_GROUP), emptied_before, freed_by)
                emptied_before = None
            for n in pair:
                if n + 2 < GROUPS:
                    multiply_on_vector(n + 2)
            scalar_turn(pair[0])
            if step < STEPS - 2:
                emptied_before = empty_on_scalar(part_sums)
            elif step == STEPS - 2:
                subtract_on_gpsimd(parts[0], empty_on_scalar(part_sums[0:1]))
                subtract_on_vector(parts[1], part_sums[1])
            else:
                for part, sums in zip(parts, part_sums):
                    subtract_on_vector(part, sums)
            scalar_turn(pair[1])
            regroup_on_tensor(planes_waiting[:-1])
